import numpy as np
import ml_dtypes


def mxq(x, axis, fmt="e4m3"):
    dtype, down = {"e4m3": (ml_dtypes.float8_e4m3fn, 7), "e5m2": (ml_dtypes.float8_e5m2, 14)}[fmt]
    v = np.moveaxis(np.asarray(x, np.float32).astype(ml_dtypes.bfloat16).astype(np.float64), axis, -1)
    blocks = v.reshape(v.shape[:-1] + (-1, 32))
    amax = np.abs(blocks).max(-1, keepdims=True)
    byte = np.maximum(np.where(amax > 0, np.frexp(amax)[1] - 1 + 127, 0) - down, 1)
    scale = np.exp2(byte - 127.0)
    codes = (blocks / scale).astype(np.float32).astype(dtype).astype(np.float64)
    return np.moveaxis((codes * scale).reshape(v.shape), -1, axis)


WIDE = False


def mx_kscale(k):
    if not WIDE:
        return np.ones(k)
    levels = np.array([10, -10, 5, -5, 0])
    if k % 512:
        return np.exp2(np.random.permutation(np.resize(levels, k // 32))).repeat(32)
    a = np.empty((k // 512, 16))
    for p in range(k // 512):
        a[p, :8] = np.random.permutation(np.resize(levels, 8))
        for g in range(8):
            far = levels[np.abs(levels - a[p, g]) >= 10]
            a[p, g + 8] = far[np.random.randint(len(far))]
    return np.exp2(a.ravel()).repeat(32)


BF16 = ml_dtypes.bfloat16


def bf(x):
    return np.asarray(x, np.float32).astype(BF16)


def f64(x):
    return np.asarray(x).astype(np.float64)


S, D, H, DH = 512, 2048, 16, 128
ROPE_BASE = 10000.0


def rotate_half(v):
    shp = v.shape
    p = v.reshape(*shp[:-1], shp[-1] // 2, 2)
    return np.stack((-p[..., 1], p[..., 0]), axis=-1).reshape(shp)


def rope_cos_sin(seq_len, dh):
    inv_freq = 1.0 / (ROPE_BASE ** (np.arange(0, dh, 2) / dh))
    t = np.arange(seq_len)
    freqs = t[:, None] * inv_freq[None, :]
    return np.repeat(np.cos(freqs), 2, axis=-1), np.repeat(np.sin(freqs), 2, axis=-1)


def setup_inputs():
    s = mx_kscale(D)
    return {"x": bf(np.random.standard_normal((S, D)) * s),
            "w": bf(np.random.standard_normal((H * DH, D)) / np.sqrt(D) / s[None, :])}


def core(x, w):
    y = mxq(f64(x), 1, "e4m3") @ mxq(f64(w), 1, "e4m3").T
    q = y.reshape(S, H, DH).transpose(1, 0, 2)
    cos, sin = rope_cos_sin(S, DH)
    return q * cos[None] + rotate_half(q) * sin[None]


def e4m3fn_bytes(y):
    return np.clip(np.asarray(y, np.float64), -448.0, 448.0).astype(np.float32).astype(ml_dtypes.float8_e4m3fn).view(np.uint8)


def reference(x, w):
    out = core(x, w)
    s = np.max(np.abs(out), axis=-1, keepdims=True) / 448.0
    return out, e4m3fn_bytes(out / s)

@@ -1,0 +1,254 @@
+from contextlib import ExitStack
+
+import concourse.mybir as mybir
+from concourse.masks import make_identity
+
+TOKENS, K, HEADS, DH = 512, 2048, 16, 128
+ROPE_BASE = 10000.0
+PI = 3.141592653589793
+FLOPS = 2 * TOKENS * K * HEADS * DH
+
+F32 = mybir.dt.float32
+BF16 = mybir.dt.bfloat16
+U32 = mybir.dt.uint32
+I32 = mybir.dt.int32
+U8 = mybir.dt.uint8
+FP8X4 = mybir.dt.float8_e4m3fn_x4
+FP8 = mybir.dt.float8_e4m3fn
+ALU = mybir.AluOpType
+ACT = mybir.ActivationFunctionType
+AX = mybir.AxisListType
+
+P = 128
+PASSES = K // (4 * P)
+TILES = TOKENS // P
+PAIRS = HEADS // 2
+UNITS = 2 * PAIRS
+FREQS = DH // 2
+BANK = 512
+
+
+def tile_attention_pa_kernel(tc, x, w, out_0, out_1):
+    nc = tc.nc
+    with ExitStack() as ctx:
+        ctx.enter_context(tc.manual_schedule())
+        const = ctx.enter_context(tc.tile_pool(name="const", bufs=1))
+        raw = ctx.enter_context(tc.tile_pool(name="raw", bufs=1))
+        keep = ctx.enter_context(tc.tile_pool(name="keep", bufs=1))
+        stage = ctx.enter_context(tc.tile_pool(name="stage", bufs=3))
+        epi = ctx.enter_context(tc.tile_pool(name="epi", bufs=4))
+        turned = ctx.enter_context(tc.psum_pool(name="turned", bufs=4))
+        sums = ctx.enter_context(tc.psum_pool(name="sums", bufs=4))
+
+        ident = const.tile([P, P], F32, name="ident")
+        make_identity(nc, ident[:])
+        zeros = const.tile([P, 1], F32, name="zeros")
+        nc.vector.memset(zeros[:], 0.0)
+        first_sin = const.tile([P, 1], F32, name="first_sin")
+        nc.scalar.activation(out=first_sin[:], in_=zeros[:], func=ACT.Sin)
+
+        x_tiles = x.rearrange("(p m) k -> m p k", m=TILES)
+        x_raw = [raw.tile([P, K], BF16, name="x%d" % m) for m in range(TILES)]
+        w_raw = [raw.tile([P, K], BF16, name="w%d" % h) for h in range(HEADS)]
+
+        def load_x(m):
+            nc.sync.dma_start(out=x_raw[m][:], in_=x_tiles[m])
+
+        def load_w(h):
+            nc.sync.dma_start(out=w_raw[h][:], in_=w[h * P:(h + 1) * P, :])
+
+        load_x(0)
+        load_x(1)
+        load_w(0)
+        load_w(1)
+        load_x(2)
+        load_x(3)
+        for h in range(2, HEADS):
+            load_w(h)
+
+        freq = const.tile([P, FREQS], F32, name="freq")
+        nc.vector.memset(freq[:, 0:1], 1.0)
+        for n in (1, 2, 4, 8, 16, 32):
+            nc.vector.tensor_scalar(out=freq[:, n:2 * n], in0=freq[:, 0:n], scalar1=ROPE_BASE ** (-n / float(FREQS)),
+                                    scalar2=None, op0=ALU.mult)
+        token_i = const.tile([P, TILES], I32, name="token_i")
+        nc.gpsimd.iota(token_i[:], pattern=[[1, TILES]], base=0, channel_multiplier=TILES)
+        token = const.tile([P, TILES], F32, name="token")
+        nc.vector.tensor_copy(out=token[:], in_=token_i[:])
+        turns = const.tile([P, 2, TILES, FREQS], F32, name="turns")
+        for m in range(TILES):
+            nc.vector.tensor_scalar(out=turns[:, 0, m, :], in0=freq[:], scalar1=token[:, m:m + 1],
+                                    scalar2=1.0 / (2.0 * PI), op0=ALU.mult, op1=ALU.mult)
+        nc.vector.tensor_scalar(out=turns[:, 1, :, :], in0=turns[:, 0, :, :], scalar1=0.25, scalar2=None, op0=ALU.add)
+        turns_flat = turns[:].rearrange("p s m n -> p (s m n)")
+        whole_i = const.tile([P, 2 * TILES * FREQS], I32, name="whole_i")
+        nc.vector.tensor_copy(out=whole_i[:], in_=turns_flat)
+        whole = const.tile([P, 2 * TILES * FREQS], F32, name="whole")
+        nc.vector.tensor_copy(out=whole[:], in_=whole_i[:])
+        rest = const.tile([P, 2 * TILES * FREQS], F32, name="rest")
+        nc.vector.tensor_tensor(out=rest[:], in0=turns_flat, in1=whole[:], op=ALU.subtract)
+        rest_neg = const.tile([P, 2 * TILES * FREQS], F32, name="rest_neg")
+        nc.vector.scalar_tensor_tensor(out=rest_neg[:], in0=rest[:], scalar=0.5, in1=rest[:], op0=ALU.is_gt,
+                                       op1=ALU.subtract)
+        sin_cos = const.tile([P, 2, TILES, FREQS], F32, name="sin_cos")
+        cos_table = const.tile([P, TILES, DH], F32, name="cos_table")
+        sin_table = const.tile([P, TILES, DH], F32, name="sin_table")
+        cos_pairs = cos_table[:].rearrange("p m (n e) -> p m n e", e=2)
+        sin_pairs = sin_table[:].rearrange("p m (n e) -> p m n e", e=2)
+
+        def take_sines():
+            nc.scalar.activation(out=sin_cos[:].rearrange("p s m n -> p (s m n)"), in_=rest_neg[:], func=ACT.Sin,
+                                 scale=-2.0 * PI)
+
+        def spread_tables():
+            for e in range(2):
+                nc.vector.tensor_copy(out=cos_pairs[:, :, :, e], in_=sin_cos[:, 1, :, :])
+                nc.vector.tensor_scalar(out=sin_pairs[:, :, :, e], in0=sin_cos[:, 0, :, :],
+                                        scalar1=(-1.0 if e == 0 else 1.0), scalar2=None, op0=ALU.mult)
+
+        def turn_two_passes(rows, gp, grouped):
+            words = rows[:].bitcast(F32)
+            bank = turned.tile([P, BANK], F32, name="bank")
+            for gl in range(2):
+                for u in range(2):
+                    g = 2 * gp + gl
+                    s = 2 * gl + u
+                    nc.tensor.transpose(bank[:, s * P:(s + 1) * P], words[:, 256 * g + u:256 * (g + 1):2], ident[:])
+            nc.scalar.copy(out=grouped, in_=bank[:].rearrange("p (g u r) -> p g r u", g=2, u=2))
+
+        x_grouped = [None] * TILES
+        x_codes = [keep.tile([P, PASSES * P], U32, name="x_codes%d" % m, align_bytes=64) for m in range(TILES)]
+        x_scales = [keep.tile([P, PASSES * P], U8, name="x_scales%d" % m, align_bytes=64) for m in range(TILES)]
+
+        def turn_x(m):
+            x_grouped[m] = stage.tile([P, K], BF16, name="x_grouped", align_bytes=64)
+            view = x_grouped[m][:].bitcast(F32).rearrange("p (g r u) -> p g r u", g=PASSES, u=2)
+            for gp in range(2):
+                turn_two_passes(x_raw[m], gp, view[:, 2 * gp:2 * gp + 2, :, :])
+
+        def quantize_x(m):
+            nc.vector.quantize_mx(out=x_codes[m][:].bitcast(FP8X4), scales=x_scales[m][:], in_=x_grouped[m][:])
+
+        w_grouped = [None] * PAIRS
+        w_codes = [None] * PAIRS
+        w_scales = [None] * PAIRS
+
+        def turn_w(hp, gp, hl):
+            if w_grouped[hp] is None:
+                w_grouped[hp] = stage.tile([P, 2 * K], BF16, name="w_grouped", align_bytes=64)
+            view = w_grouped[hp][:].bitcast(F32).rearrange("p (g h d u) -> p g h d u", g=PASSES, h=2, u=2)
+            turn_two_passes(w_raw[2 * hp + hl], gp, view[:, 2 * gp:2 * gp + 2, hl, :, :])
+
+        def turn_half(q):
+            for hl in range(2):
+                turn_w(q // 2, q % 2, hl)
+
+        def quantize_half(q):
+            hp, gp = q // 2, q % 2
+            if w_codes[hp] is None:
+                w_codes[hp] = stage.tile([P, PASSES * 2 * DH], U32, name="w_codes", align_bytes=64)
+                w_scales[hp] = stage.tile([P, PASSES * 2 * DH], U8, name="w_scales", align_bytes=64)
+            cols = slice(gp * BANK, (gp + 1) * BANK)
+            nc.vector.quantize_mx(out=w_codes[hp][:, cols].bitcast(FP8X4), scales=w_scales[hp][:, cols],
+                                  in_=w_grouped[hp][:, gp * K:(gp + 1) * K])
+
+        out0_rows = out_0.rearrange("h (p m) d -> p h m d", m=TILES)
+        out1_rows = out_1.rearrange("h (p m) d -> p h m d", m=TILES)
+        acc = [None] * UNITS
+        by_cos = [None] * UNITS
+        rotated = [None] * UNITS
+        row_amax = [None] * UNITS
+
+        def multiply(u):
+            hp, mp = u // 2, u % 2
+            acc[u] = sums.tile([P, BANK], F32, name="acc")
+            for ml in range(2):
+                m = 2 * mp + ml
+                for g in range(PASSES):
+                    nc.tensor.matmul_mx(out=acc[u][:, ml * 2 * DH:(ml + 1) * 2 * DH],
+                                        lhsT=x_codes[m][:, g * P:(g + 1) * P].bitcast(FP8X4),
+                                        lhsT_scale=x_scales[m][:, g * P:(g + 1) * P],
+                                        rhs=w_codes[hp][:, g * 2 * DH:(g + 1) * 2 * DH].bitcast(FP8X4),
+                                        rhs_scale=w_scales[hp][:, g * 2 * DH:(g + 1) * 2 * DH],
+                                        start=(g == 0), stop=(g == PASSES - 1))
+
+        def times_cos(u):
+            mp = u % 2
+            by_cos[u] = epi.tile([P, BANK], F32, name="by_cos")
+            nc.vector.tensor_tensor(out=by_cos[u][:].rearrange("p (m h d) -> p m h d", m=2, h=2),
+                                    in0=acc[u][:].rearrange("p (m h d) -> p m h d", m=2, h=2),
+                                    in1=cos_table[:, 2 * mp:2 * mp + 2, :].unsqueeze(2).to_broadcast([P, 2, 2, DH]),
+                                    op=ALU.mult)
+
+        def times_sin_and_add(u):
+            hp, mp = u // 2, u % 2
+            by_sin = epi.tile([P, BANK], F32, name="by_sin")
+            nc.vector.tensor_tensor(
+                out=by_sin[:].rearrange("p (m h n e) -> p m h n e", m=2, h=2, e=2),
+                in0=acc[u][:].rearrange("p (m h n e) -> p m h n e", m=2, h=2, e=2)[:, :, :, :, ::-1],
+                in1=sin_pairs[:, 2 * mp:2 * mp + 2, :, :].unsqueeze(2).to_broadcast([P, 2, 2, FREQS, 2]),
+                op=ALU.mult)
+            rotated[u] = epi.tile([P, BANK], F32, name="rotated")
+            nc.gpsimd.tensor_tensor(out=rotated[u][:].rearrange("p (h m d) -> p m h d", h=2, m=2),
+                                    in0=by_cos[u][:].rearrange("p (m h d) -> p m h d", m=2, h=2),
+                                    in1=by_sin[:].rearrange("p (m h d) -> p m h d", m=2, h=2), op=ALU.add)
+            nc.sync.dma_start(out=out0_rows[:, 2 * hp:2 * hp + 2, 2 * mp:2 * mp + 2, :],
+                              in_=rotated[u][:].rearrange("p (h m d) -> p h m d", h=2, m=2))
+
+        def take_row_amax(u):
+            row_amax[u] = epi.tile([P, 4], F32, name="row_amax")
+            nc.vector.tensor_reduce(out=row_amax[u][:], in_=rotated[u][:].rearrange("p (r d) -> p r d", d=DH),
+                                    axis=AX.X, op=ALU.max, apply_absolute_value=True)
+
+        def cast_and_store(u, rows_on_vector):
+            hp, mp = u // 2, u % 2
+            inverse = epi.tile([P, 4], F32, name="inverse")
+            nc.vector.reciprocal(out=inverse[:], in_=row_amax[u][:])
+            factor = epi.tile([P, 4], F32, name="factor")
+            nc.scalar.activation(out=factor[:], in_=inverse[:], func=ACT.Copy, scale=448.0)
+            codes = epi.tile([P, BANK], FP8, name="codes")
+            for r in range(4):
+                cols = slice(r * DH, (r + 1) * DH)
+                if r >= 4 - rows_on_vector:
+                    nc.vector.tensor_scalar(out=codes[:, cols], in0=rotated[u][:, cols], scalar1=factor[:, r:r + 1],
+                                            scalar2=None, op0=ALU.mult, saturate=False)
+                else:
+                    nc.scalar.activation(out=codes[:, cols], in_=rotated[u][:, cols], func=ACT.Identity,
+                                         scale=factor[:, r:r + 1], bias=zeros[:, 0:1], saturate=False)
+            nc.sync.dma_start(out=out1_rows[:, 2 * hp:2 * hp + 2, 2 * mp:2 * mp + 2, :],
+                              in_=codes[:].bitcast(U8).rearrange("p (h m d) -> p h m d", h=2, m=2))
+
+        turn_x(0)
+        turn_x(1)
+        quantize_x(0)
+        take_sines()
+        quantize_x(1)
+        for hl in range(2):
+            for gp in range(2):
+                turn_w(0, gp, hl)
+        spread_tables()
+        quantize_half(0)
+        quantize_half(1)
+        turn_x(2)
+        quantize_x(2)
+        turn_x(3)
+        multiply(0)
+        quantize_x(3)
+        turn_half(2)
+
+        for u in range(UNITS):
+            if u + 3 < UNITS:
+                turn_half(u + 3)
+            times_cos(u)
+            if u + 2 < UNITS:
+                quantize_half(u + 2)
+            if u + 1 < UNITS:
+                multiply(u + 1)
+            times_sin_and_add(u)
+            if u >= 1:
+                take_row_amax(u - 1)
+            if u >= 2:
+                cast_and_store(u - 2, 0)
+        cast_and_store(UNITS - 2, 0)
+        take_row_amax(UNITS - 1)
+        cast_and_store(UNITS - 1, 2)

@@ -36,7 +36,7 @@ def tile_attention_pa_kernel(tc, x, w, out_0, out_1):
         raw = ctx.enter_context(tc.tile_pool(name="raw", bufs=1))
         keep = ctx.enter_context(tc.tile_pool(name="keep", bufs=1))
         stage = ctx.enter_context(tc.tile_pool(name="stage", bufs=3))
-        epi = ctx.enter_context(tc.tile_pool(name="epi", bufs=4))
+        epi = ctx.enter_context(tc.tile_pool(name="epi", bufs=5))
         turned = ctx.enter_context(tc.psum_pool(name="turned", bufs=4))
         sums = ctx.enter_context(tc.psum_pool(name="sums", bufs=4))
 
@@ -91,20 +91,20 @@ def tile_attention_pa_kernel(tc, x, w, out_0, out_1):
         nc.vector.scalar_tensor_tensor(out=rest_neg[:], in0=rest[:], scalar=0.5, in1=rest[:], op0=ALU.is_gt,
                                        op1=ALU.subtract)
         sin_cos = const.tile([P, 2, TILES, FREQS], F32, name="sin_cos")
-        cos_table = const.tile([P, TILES, DH], F32, name="cos_table")
-        sin_table = const.tile([P, TILES, DH], F32, name="sin_table")
-        cos_pairs = cos_table[:].rearrange("p m (n e) -> p m n e", e=2)
-        sin_pairs = sin_table[:].rearrange("p m (n e) -> p m n e", e=2)
+        both = [const.tile([P, 2, 2, 2, DH], F32, name="both%d" % mp) for mp in range(2)]
 
         def take_sines():
             nc.scalar.activation(out=sin_cos[:].rearrange("p s m n -> p (s m n)"), in_=rest_neg[:], func=ACT.Sin,
                                  scale=-2.0 * PI)
 
-        def spread_tables():
-            for e in range(2):
-                nc.vector.tensor_copy(out=cos_pairs[:, :, :, e], in_=sin_cos[:, 1, :, :])
-                nc.vector.tensor_scalar(out=sin_pairs[:, :, :, e], in0=sin_cos[:, 0, :, :],
-                                        scalar1=(-1.0 if e == 0 else 1.0), scalar2=None, op0=ALU.mult)
+        def spread_tables(mp, eng):
+            for s in range(2):
+                for e in range(2):
+                    sign = -1.0 if (s == 1 and e == 1) else 1.0
+                    eng.tensor_scalar(
+                        out=both[mp][:, s, :, :, :].rearrange("p m h (n e) -> p m h n e", e=2)[:, :, :, :, e],
+                        in0=sin_cos[:, 1 - s, 2 * mp:2 * mp + 2, :].unsqueeze(2).to_broadcast([P, 2, 2, FREQS]),
+                        scalar1=sign, scalar2=0.0, op0=ALU.mult, op1=ALU.add)
 
         def turn_two_passes(rows, gp, grouped):
             words = rows[:].bitcast(F32)
@@ -143,21 +143,19 @@ def tile_attention_pa_kernel(tc, x, w, out_0, out_1):
             for hl in range(2):
                 turn_w(q // 2, q % 2, hl)
 
-        def quantize_half(q):
-            hp, gp = q // 2, q % 2
-            if w_codes[hp] is None:
-                w_codes[hp] = stage.tile([P, PASSES * 2 * DH], U32, name="w_codes", align_bytes=64)
-                w_scales[hp] = stage.tile([P, PASSES * 2 * DH], U8, name="w_scales", align_bytes=64)
-            cols = slice(gp * BANK, (gp + 1) * BANK)
-            nc.vector.quantize_mx(out=w_codes[hp][:, cols].bitcast(FP8X4), scales=w_scales[hp][:, cols],
-                                  in_=w_grouped[hp][:, gp * K:(gp + 1) * K])
+        def quantize_pair(hp):
+            w_codes[hp] = stage.tile([P, PASSES * 2 * DH], U32, name="w_codes", align_bytes=64)
+            w_scales[hp] = stage.tile([P, PASSES * 2 * DH], U8, name="w_scales", align_bytes=64)
+            nc.vector.quantize_mx(out=w_codes[hp][:].bitcast(FP8X4), scales=w_scales[hp][:], in_=w_grouped[hp][:])
 
         out0_rows = out_0.rearrange("h (p m) d -> p h m d", m=TILES)
         out1_rows = out_1.rearrange("h (p m) d -> p h m d", m=TILES)
         acc = [None] * UNITS
-        by_cos = [None] * UNITS
-        rotated = [None] * UNITS
-        row_amax = [None] * UNITS
+        prod = [None] * UNITS
+        rot = [None] * PAIRS
+        row_amax = [None] * PAIRS
+        factor = [None] * PAIRS
+        codes = [None] * PAIRS
 
         def multiply(u):
             hp, mp = u // 2, u % 2
@@ -172,83 +170,163 @@ def tile_attention_pa_kernel(tc, x, w, out_0, out_1):
                                         rhs_scale=w_scales[hp][:, g * 2 * DH:(g + 1) * 2 * DH],
                                         start=(g == 0), stop=(g == PASSES - 1))
 
-        def times_cos(u):
-            mp = u % 2
-            by_cos[u] = epi.tile([P, BANK], F32, name="by_cos")
-            nc.vector.tensor_tensor(out=by_cos[u][:].rearrange("p (m h d) -> p m h d", m=2, h=2),
-                                    in0=acc[u][:].rearrange("p (m h d) -> p m h d", m=2, h=2),
-                                    in1=cos_table[:, 2 * mp:2 * mp + 2, :].unsqueeze(2).to_broadcast([P, 2, 2, DH]),
-                                    op=ALU.mult)
+        def products(u):
+            prod[u] = epi.tile([P, 2, BANK], F32, name="prod")
+            nc.vector.tensor_tensor(out=prod[u][:], in0=acc[u][:].unsqueeze(1).to_broadcast([P, 2, BANK]),
+                                    in1=both[u % 2][:].rearrange("p s m h d -> p s (m h d)"), op=ALU.mult)
 
-        def times_sin_and_add(u):
+        def add_and_store(u, eng):
             hp, mp = u // 2, u % 2
-            by_sin = epi.tile([P, BANK], F32, name="by_sin")
-            nc.vector.tensor_tensor(
-                out=by_sin[:].rearrange("p (m h n e) -> p m h n e", m=2, h=2, e=2),
-                in0=acc[u][:].rearrange("p (m h n e) -> p m h n e", m=2, h=2, e=2)[:, :, :, :, ::-1],
-                in1=sin_pairs[:, 2 * mp:2 * mp + 2, :, :].unsqueeze(2).to_broadcast([P, 2, 2, FREQS, 2]),
-                op=ALU.mult)
-            rotated[u] = epi.tile([P, BANK], F32, name="rotated")
-            nc.gpsimd.tensor_tensor(out=rotated[u][:].rearrange("p (h m d) -> p m h d", h=2, m=2),
-                                    in0=by_cos[u][:].rearrange("p (m h d) -> p m h d", m=2, h=2),
-                                    in1=by_sin[:].rearrange("p (m h d) -> p m h d", m=2, h=2), op=ALU.add)
+            if rot[hp] is None:
+                rot[hp] = epi.tile([P, 2, BANK], F32, name="rot")
+            eng.tensor_tensor(out=rot[hp][:, mp, :].rearrange("p (h m n e) -> p m h n e", h=2, m=2, e=2),
+                              in0=prod[u][:, 0, :].rearrange("p (m h n e) -> p m h n e", m=2, h=2, e=2),
+                              in1=prod[u][:, 1, :].rearrange("p (m h n e) -> p m h n e", m=2, h=2, e=2)[:, :, :, :, ::-1],
+                              op=ALU.add)
             nc.sync.dma_start(out=out0_rows[:, 2 * hp:2 * hp + 2, 2 * mp:2 * mp + 2, :],
-                              in_=rotated[u][:].rearrange("p (h m d) -> p h m d", h=2, m=2))
+                              in_=rot[hp][:, mp, :].rearrange("p (h m d) -> p h m d", h=2, m=2))
 
-        def take_row_amax(u):
-            row_amax[u] = epi.tile([P, 4], F32, name="row_amax")
-            nc.vector.tensor_reduce(out=row_amax[u][:], in_=rotated[u][:].rearrange("p (r d) -> p r d", d=DH),
+        def take_row_amax(hp, lo, n):
+            if row_amax[hp] is None:
+                row_amax[hp] = epi.tile([P, 8], F32, name="row_amax")
+                factor[hp] = epi.tile([P, 8], F32, name="factor")
+            nc.vector.tensor_reduce(out=row_amax[hp][:, lo:lo + n],
+                                    in_=rot[hp][:].rearrange("p u (r d) -> p (u r) d", d=DH)[:, lo:lo + n, :],
                                     axis=AX.X, op=ALU.max, apply_absolute_value=True)
+            inverse = epi.tile([P, 8], F32, name="inverse")
+            nc.vector.reciprocal(out=inverse[:, lo:lo + n], in_=row_amax[hp][:, lo:lo + n])
+            nc.scalar.activation(out=factor[hp][:, lo:lo + n], in_=inverse[:, lo:lo + n], func=ACT.Copy, scale=448.0)
 
-        def cast_and_store(u, rows_on_vector):
-            hp, mp = u // 2, u % 2
-            inverse = epi.tile([P, 4], F32, name="inverse")
-            nc.vector.reciprocal(out=inverse[:], in_=row_amax[u][:])
-            factor = epi.tile([P, 4], F32, name="factor")
-            nc.scalar.activation(out=factor[:], in_=inverse[:], func=ACT.Copy, scale=448.0)
-            codes = epi.tile([P, BANK], FP8, name="codes")
-            for r in range(4):
+        def cast_rows(hp, lo, n, on_vector):
+            if codes[hp] is None:
+                codes[hp] = epi.tile([P, 2 * BANK], FP8, name="codes")
+            flat = rot[hp][:].rearrange("p u c -> p (u c)")
+            for r in range(lo, lo + n):
                 cols = slice(r * DH, (r + 1) * DH)
-                if r >= 4 - rows_on_vector:
-                    nc.vector.tensor_scalar(out=codes[:, cols], in0=rotated[u][:, cols], scalar1=factor[:, r:r + 1],
+                if r >= lo + n - on_vector:
+                    nc.vector.tensor_scalar(out=codes[hp][:, cols], in0=flat[:, cols], scalar1=factor[hp][:, r:r + 1],
                                             scalar2=None, op0=ALU.mult, saturate=False)
                 else:
-                    nc.scalar.activation(out=codes[:, cols], in_=rotated[u][:, cols], func=ACT.Identity,
-                                         scale=factor[:, r:r + 1], bias=zeros[:, 0:1], saturate=False)
-            nc.sync.dma_start(out=out1_rows[:, 2 * hp:2 * hp + 2, 2 * mp:2 * mp + 2, :],
-                              in_=codes[:].bitcast(U8).rearrange("p (h m d) -> p h m d", h=2, m=2))
+                    nc.scalar.activation(out=codes[hp][:, cols], in_=flat[:, cols], func=ACT.Identity,
+                                         scale=factor[hp][:, r:r + 1], bias=zeros[:, 0:1], saturate=False)
+
+        def store_codes(hp, mp, n):
+            for q in range(mp, mp + n):
+                nc.sync.dma_start(out=out1_rows[:, 2 * hp:2 * hp + 2, 2 * q:2 * q + 2, :],
+                                  in_=codes[hp][:, q * BANK:(q + 1) * BANK].bitcast(U8).rearrange("p (h m d) -> p h m d", h=2, m=2))
 
         turn_x(0)
         turn_x(1)
         quantize_x(0)
         take_sines()
         quantize_x(1)
-        for hl in range(2):
-            for gp in range(2):
-                turn_w(0, gp, hl)
-        spread_tables()
-        quantize_half(0)
-        quantize_half(1)
+        turn_w(0, 0, 0)
+        turn_w(0, 1, 0)
+        turn_w(0, 0, 1)
+        turn_w(0, 1, 1)
+        spread_tables(0, nc.vector)
+        quantize_pair(0)
         turn_x(2)
         quantize_x(2)
         turn_x(3)
         multiply(0)
         quantize_x(3)
+        spread_tables(1, nc.gpsimd)
         turn_half(2)
-
-        for u in range(UNITS):
-            if u + 3 < UNITS:
-                turn_half(u + 3)
-            times_cos(u)
-            if u + 2 < UNITS:
-                quantize_half(u + 2)
-            if u + 1 < UNITS:
-                multiply(u + 1)
-            times_sin_and_add(u)
-            if u >= 1:
-                take_row_amax(u - 1)
-            if u >= 2:
-                cast_and_store(u - 2, 0)
-        cast_and_store(UNITS - 2, 0)
-        take_row_amax(UNITS - 1)
-        cast_and_store(UNITS - 1, 2)
+        turn_half(3)
+        products(0)
+        add_and_store(0, nc.gpsimd)
+        multiply(1)
+        quantize_pair(1)
+        turn_half(4)
+        turn_half(5)
+        products(1)
+        add_and_store(1, nc.gpsimd)
+        multiply(2)
+        multiply(3)
+        take_row_amax(0, 0, 8)
+        cast_rows(0, 0, 8, 0)
+        store_codes(0, 0, 2)
+        quantize_pair(2)
+        turn_half(6)
+        turn_half(7)
+        products(2)
+        add_and_store(2, nc.gpsimd)
+        products(3)
+        add_and_store(3, nc.gpsimd)
+        multiply(4)
+        multiply(5)
+        quantize_pair(3)
+        turn_half(8)
+        turn_half(9)
+        products(4)
+        add_and_store(4, nc.gpsimd)
+        products(5)
+        add_and_store(5, nc.gpsimd)
+        multiply(6)
+        multiply(7)
+        take_row_amax(1, 0, 8)
+        cast_rows(1, 0, 8, 0)
+        store_codes(1, 0, 2)
+        quantize_pair(4)
+        turn_half(10)
+        turn_half(11)
+        products(6)
+        add_and_store(6, nc.gpsimd)
+        products(7)
+        add_and_store(7, nc.gpsimd)
+        multiply(8)
+        multiply(9)
+        take_row_amax(2, 0, 8)
+        cast_rows(2, 0, 8, 0)
+        store_codes(2, 0, 2)
+        quantize_pair(5)
+        turn_half(12)
+        turn_half(13)
+        products(8)
+        add_and_store(8, nc.gpsimd)
+        products(9)
+        add_and_store(9, nc.gpsimd)
+        multiply(10)
+        multiply(11)
+        take_row_amax(3, 0, 8)
+        cast_rows(3, 0, 8, 0)
+        store_codes(3, 0, 2)
+        quantize_pair(6)
+        turn_half(14)
+        turn_half(15)
+        products(10)
+        add_and_store(10, nc.gpsimd)
+        products(11)
+        add_and_store(11, nc.gpsimd)
+        multiply(12)
+        multiply(13)
+        take_row_amax(4, 0, 8)
+        cast_rows(4, 0, 8, 0)
+        store_codes(4, 0, 2)
+        quantize_pair(7)
+        multiply(14)
+        multiply(15)
+        products(12)
+        add_and_store(12, nc.gpsimd)
+        products(13)
+        add_and_store(13, nc.gpsimd)
+        take_row_amax(5, 0, 8)
+        cast_rows(5, 0, 8, 0)
+        store_codes(5, 0, 2)
+        products(14)
+        add_and_store(14, nc.gpsimd)
+        take_row_amax(6, 0, 4)
+        cast_rows(6, 0, 4, 0)
+        store_codes(6, 0, 1)
+        products(15)
+        add_and_store(15, nc.gpsimd)
+        take_row_amax(6, 4, 4)
+        cast_rows(6, 4, 4, 0)
+        store_codes(6, 1, 1)
+        take_row_amax(7, 0, 4)
+        cast_rows(7, 0, 4, 0)
+        store_codes(7, 0, 1)
+        take_row_amax(7, 4, 4)
+        cast_rows(7, 4, 4, 2)
+        store_codes(7, 1, 1)

@@ -36,7 +36,7 @@ def tile_attention_pa_kernel(tc, x, w, out_0, out_1):
         raw = ctx.enter_context(tc.tile_pool(name="raw", bufs=1))
         keep = ctx.enter_context(tc.tile_pool(name="keep", bufs=1))
         stage = ctx.enter_context(tc.tile_pool(name="stage", bufs=3))
-        epi = ctx.enter_context(tc.tile_pool(name="epi", bufs=5))
+        epi = ctx.enter_context(tc.tile_pool(name="epi", bufs=6))
         turned = ctx.enter_context(tc.psum_pool(name="turned", bufs=4))
         sums = ctx.enter_context(tc.psum_pool(name="sums", bufs=4))
 
@@ -143,10 +143,13 @@ def tile_attention_pa_kernel(tc, x, w, out_0, out_1):
             for hl in range(2):
                 turn_w(q // 2, q % 2, hl)
 
-        def quantize_pair(hp):
-            w_codes[hp] = stage.tile([P, PASSES * 2 * DH], U32, name="w_codes", align_bytes=64)
-            w_scales[hp] = stage.tile([P, PASSES * 2 * DH], U8, name="w_scales", align_bytes=64)
-            nc.vector.quantize_mx(out=w_codes[hp][:].bitcast(FP8X4), scales=w_scales[hp][:], in_=w_grouped[hp][:])
+        def quantize_passes(hp, first, count):
+            if w_codes[hp] is None:
+                w_codes[hp] = stage.tile([P, PASSES * 2 * DH], U32, name="w_codes", align_bytes=64)
+                w_scales[hp] = stage.tile([P, PASSES * 2 * DH], U8, name="w_scales", align_bytes=64)
+            cols = slice(first * 2 * DH, (first + count) * 2 * DH)
+            nc.vector.quantize_mx(out=w_codes[hp][:, cols].bitcast(FP8X4), scales=w_scales[hp][:, cols],
+                                  in_=w_grouped[hp][:, first * 8 * DH:(first + count) * 8 * DH])
 
         out0_rows = out_0.rearrange("h (p m) d -> p h m d", m=TILES)
         out1_rows = out_1.rearrange("h (p m) d -> p h m d", m=TILES)
@@ -193,6 +196,8 @@ def tile_attention_pa_kernel(tc, x, w, out_0, out_1):
             nc.vector.tensor_reduce(out=row_amax[hp][:, lo:lo + n],
                                     in_=rot[hp][:].rearrange("p u (r d) -> p (u r) d", d=DH)[:, lo:lo + n, :],
                                     axis=AX.X, op=ALU.max, apply_absolute_value=True)
+
+        def make_factor(hp, lo, n):
             inverse = epi.tile([P, 8], F32, name="inverse")
             nc.vector.reciprocal(out=inverse[:, lo:lo + n], in_=row_amax[hp][:, lo:lo + n])
             nc.scalar.activation(out=factor[hp][:, lo:lo + n], in_=inverse[:, lo:lo + n], func=ACT.Copy, scale=448.0)
@@ -225,7 +230,8 @@ def tile_attention_pa_kernel(tc, x, w, out_0, out_1):
         turn_w(0, 0, 1)
         turn_w(0, 1, 1)
         spread_tables(0, nc.vector)
-        quantize_pair(0)
+        quantize_passes(0, 0, 2)
+        quantize_passes(0, 2, 2)
         turn_x(2)
         quantize_x(2)
         turn_x(3)
@@ -233,100 +239,121 @@ def tile_attention_pa_kernel(tc, x, w, out_0, out_1):
         quantize_x(3)
         spread_tables(1, nc.gpsimd)
         turn_half(2)
-        turn_half(3)
         products(0)
         add_and_store(0, nc.gpsimd)
+        quantize_passes(1, 0, 2)
+        turn_half(3)
         multiply(1)
-        quantize_pair(1)
         turn_half(4)
         turn_half(5)
-        products(1)
-        add_and_store(1, nc.gpsimd)
+        quantize_passes(1, 2, 2)
         multiply(2)
         multiply(3)
-        take_row_amax(0, 0, 8)
-        cast_rows(0, 0, 8, 0)
-        store_codes(0, 0, 2)
-        quantize_pair(2)
+        products(1)
+        add_and_store(1, nc.gpsimd)
+        take_row_amax(0, 0, 4)
+        quantize_passes(2, 0, 2)
         turn_half(6)
         turn_half(7)
-        products(2)
-        add_and_store(2, nc.gpsimd)
-        products(3)
-        add_and_store(3, nc.gpsimd)
+        quantize_passes(2, 2, 2)
         multiply(4)
         multiply(5)
-        quantize_pair(3)
+        make_factor(0, 0, 4)
+        products(2)
+        add_and_store(2, nc.gpsimd)
+        take_row_amax(0, 4, 4)
+        cast_rows(0, 0, 4, 0)
+        store_codes(0, 0, 1)
+        quantize_passes(3, 0, 2)
+        make_factor(0, 4, 4)
+        products(3)
+        add_and_store(3, nc.gpsimd)
+        take_row_amax(1, 0, 4)
+        cast_rows(0, 4, 4, 0)
+        store_codes(0, 1, 1)
         turn_half(8)
         turn_half(9)
-        products(4)
-        add_and_store(4, nc.gpsimd)
-        products(5)
-        add_and_store(5, nc.gpsimd)
+        quantize_passes(3, 2, 2)
         multiply(6)
         multiply(7)
-        take_row_amax(1, 0, 8)
-        cast_rows(1, 0, 8, 0)
-        store_codes(1, 0, 2)
-        quantize_pair(4)
+        make_factor(1, 0, 4)
+        products(4)
+        add_and_store(4, nc.gpsimd)
+        take_row_amax(1, 4, 4)
+        cast_rows(1, 0, 4, 0)
+        store_codes(1, 0, 1)
+        products(5)
+        add_and_store(5, nc.gpsimd)
+        make_factor(1, 4, 4)
+        cast_rows(1, 4, 4, 0)
+        store_codes(1, 1, 1)
+        quantize_passes(4, 0, 4)
         turn_half(10)
         turn_half(11)
+        multiply(8)
+        multiply(9)
         products(6)
         add_and_store(6, nc.gpsimd)
         products(7)
         add_and_store(7, nc.gpsimd)
-        multiply(8)
-        multiply(9)
         take_row_amax(2, 0, 8)
-        cast_rows(2, 0, 8, 0)
-        store_codes(2, 0, 2)
-        quantize_pair(5)
+        quantize_passes(5, 0, 4)
         turn_half(12)
         turn_half(13)
-        products(8)
-        add_and_store(8, nc.gpsimd)
-        products(9)
-        add_and_store(9, nc.gpsimd)
         multiply(10)
         multiply(11)
+        products(8)
+        add_and_store(8, nc.gpsimd)
+        make_factor(2, 0, 8)
+        cast_rows(2, 0, 8, 0)
+        store_codes(2, 0, 2)
+        products(9)
+        add_and_store(9, nc.gpsimd)
         take_row_amax(3, 0, 8)
-        cast_rows(3, 0, 8, 0)
-        store_codes(3, 0, 2)
-        quantize_pair(6)
+        quantize_passes(6, 0, 4)
         turn_half(14)
         turn_half(15)
-        products(10)
-        add_and_store(10, nc.gpsimd)
-        products(11)
-        add_and_store(11, nc.gpsimd)
         multiply(12)
         multiply(13)
+        products(10)
+        add_and_store(10, nc.gpsimd)
+        make_factor(3, 0, 8)
+        cast_rows(3, 0, 8, 0)
+        store_codes(3, 0, 2)
+        products(11)
+        add_and_store(11, nc.gpsimd)
         take_row_amax(4, 0, 8)
-        cast_rows(4, 0, 8, 0)
-        store_codes(4, 0, 2)
-        quantize_pair(7)
+        quantize_passes(7, 0, 4)
         multiply(14)
         multiply(15)
         products(12)
         add_and_store(12, nc.gpsimd)
+        make_factor(4, 0, 8)
+        cast_rows(4, 0, 8, 0)
+        store_codes(4, 0, 2)
         products(13)
         add_and_store(13, nc.gpsimd)
         take_row_amax(5, 0, 8)
-        cast_rows(5, 0, 8, 0)
-        store_codes(5, 0, 2)
         products(14)
         add_and_store(14, nc.gpsimd)
+        make_factor(5, 0, 8)
+        cast_rows(5, 0, 8, 0)
+        store_codes(5, 0, 2)
         take_row_amax(6, 0, 4)
-        cast_rows(6, 0, 4, 0)
-        store_codes(6, 0, 1)
         products(15)
         add_and_store(15, nc.gpsimd)
+        make_factor(6, 0, 4)
+        cast_rows(6, 0, 4, 0)
+        store_codes(6, 0, 1)
         take_row_amax(6, 4, 4)
+        take_row_amax(7, 0, 4)
+        make_factor(6, 4, 4)
         cast_rows(6, 4, 4, 0)
         store_codes(6, 1, 1)
-        take_row_amax(7, 0, 4)
+        make_factor(7, 0, 4)
         cast_rows(7, 0, 4, 0)
         store_codes(7, 0, 1)
         take_row_amax(7, 4, 4)
+        make_factor(7, 4, 4)
         cast_rows(7, 4, 4, 2)
         store_codes(7, 1, 1)

@@ -251,42 +251,29 @@ def tile_attention_pa_kernel(tc, x, w, out_0, out_1):
         multiply(3)
         products(1)
         add_and_store(1, nc.gpsimd)
-        take_row_amax(0, 0, 4)
-        quantize_passes(2, 0, 2)
+        quantize_passes(2, 0, 4)
         turn_half(6)
         turn_half(7)
-        quantize_passes(2, 2, 2)
         multiply(4)
         multiply(5)
-        make_factor(0, 0, 4)
         products(2)
         add_and_store(2, nc.gpsimd)
-        take_row_amax(0, 4, 4)
-        cast_rows(0, 0, 4, 0)
-        store_codes(0, 0, 1)
-        quantize_passes(3, 0, 2)
-        make_factor(0, 4, 4)
         products(3)
         add_and_store(3, nc.gpsimd)
-        take_row_amax(1, 0, 4)
-        cast_rows(0, 4, 4, 0)
-        store_codes(0, 1, 1)
+        take_row_amax(0, 0, 8)
+        quantize_passes(3, 0, 4)
         turn_half(8)
         turn_half(9)
-        quantize_passes(3, 2, 2)
         multiply(6)
         multiply(7)
-        make_factor(1, 0, 4)
         products(4)
         add_and_store(4, nc.gpsimd)
-        take_row_amax(1, 4, 4)
-        cast_rows(1, 0, 4, 0)
-        store_codes(1, 0, 1)
+        make_factor(0, 0, 8)
+        cast_rows(0, 0, 8, 0)
+        store_codes(0, 0, 2)
         products(5)
         add_and_store(5, nc.gpsimd)
-        make_factor(1, 4, 4)
-        cast_rows(1, 4, 4, 0)
-        store_codes(1, 1, 1)
+        take_row_amax(1, 0, 8)
         quantize_passes(4, 0, 4)
         turn_half(10)
         turn_half(11)
@@ -294,6 +281,9 @@ def tile_attention_pa_kernel(tc, x, w, out_0, out_1):
         multiply(9)
         products(6)
         add_and_store(6, nc.gpsimd)
+        make_factor(1, 0, 8)
+        cast_rows(1, 0, 8, 0)
+        store_codes(1, 0, 2)
         products(7)
         add_and_store(7, nc.gpsimd)
         take_row_amax(2, 0, 8)

@@ -34,6 +34,7 @@ def tile_attention_pa_kernel(tc, x, w, out_0, out_1):
         ctx.enter_context(tc.manual_schedule())
         const = ctx.enter_context(tc.tile_pool(name="const", bufs=1))
         raw = ctx.enter_context(tc.tile_pool(name="raw", bufs=1))
+        srt = ctx.enter_context(tc.tile_pool(name="srt", bufs=1))
         keep = ctx.enter_context(tc.tile_pool(name="keep", bufs=1))
         stage = ctx.enter_context(tc.tile_pool(name="stage", bufs=3))
         epi = ctx.enter_context(tc.tile_pool(name="epi", bufs=6))
@@ -106,14 +107,25 @@ def tile_attention_pa_kernel(tc, x, w, out_0, out_1):
                         in0=sin_cos[:, 1 - s, 2 * mp:2 * mp + 2, :].unsqueeze(2).to_broadcast([P, 2, 2, FREQS]),
                         scalar1=sign, scalar2=0.0, op0=ALU.mult, op1=ALU.add)
 
-        def turn_two_passes(rows, gp, grouped):
+        sorted_words = [None] * HEADS
+
+        def sort_words(h):
+            sorted_words[h] = srt.tile([P, K // 2], F32, name="sorted%d" % h)
+            nc.vector.tensor_copy(out=sorted_words[h][:].rearrange("p (g u j) -> p g u j", g=PASSES, u=2),
+                                  in_=w_raw[h][:].bitcast(F32).rearrange("p (g j u) -> p g u j", g=PASSES, u=2))
+
+        def turn_two_passes(rows, gp, grouped, presorted=None):
             words = rows[:].bitcast(F32)
             bank = turned.tile([P, BANK], F32, name="bank")
             for gl in range(2):
                 for u in range(2):
                     g = 2 * gp + gl
                     s = 2 * gl + u
-                    nc.tensor.transpose(bank[:, s * P:(s + 1) * P], words[:, 256 * g + u:256 * (g + 1):2], ident[:])
+                    if presorted is None:
+                        nc.tensor.transpose(bank[:, s * P:(s + 1) * P], words[:, 256 * g + u:256 * (g + 1):2], ident[:])
+                    else:
+                        nc.tensor.transpose(bank[:, s * P:(s + 1) * P],
+                                            presorted[:, 256 * g + P * u:256 * g + P * (u + 1)], ident[:])
             nc.scalar.copy(out=grouped, in_=bank[:].rearrange("p (g u r) -> p g r u", g=2, u=2))
 
         x_grouped = [None] * TILES
@@ -137,7 +149,7 @@ def tile_attention_pa_kernel(tc, x, w, out_0, out_1):
             if w_grouped[hp] is None:
                 w_grouped[hp] = stage.tile([P, 2 * K], BF16, name="w_grouped", align_bytes=64)
             view = w_grouped[hp][:].bitcast(F32).rearrange("p (g h d u) -> p g h d u", g=PASSES, h=2, u=2)
-            turn_two_passes(w_raw[2 * hp + hl], gp, view[:, 2 * gp:2 * gp + 2, hl, :, :])
+            turn_two_passes(w_raw[2 * hp + hl], gp, view[:, 2 * gp:2 * gp + 2, hl, :, :], sorted_words[2 * hp + hl])
 
         def turn_half(q):
             for hl in range(2):
@@ -241,6 +253,8 @@ def tile_attention_pa_kernel(tc, x, w, out_0, out_1):
         turn_half(2)
         products(0)
         add_and_store(0, nc.gpsimd)
+        sort_words(4)
+        sort_words(5)
         quantize_passes(1, 0, 2)
         turn_half(3)
         multiply(1)

@@ -265,6 +265,8 @@ def tile_attention_pa_kernel(tc, x, w, out_0, out_1):
         multiply(3)
         products(1)
         add_and_store(1, nc.gpsimd)
+        sort_words(6)
+        sort_words(7)
         quantize_passes(2, 0, 4)
         turn_half(6)
         turn_half(7)

@@ -34,10 +34,11 @@ def tile_attention_pa_kernel(tc, x, w, out_0, out_1):
         ctx.enter_context(tc.manual_schedule())
         const = ctx.enter_context(tc.tile_pool(name="const", bufs=1))
         raw = ctx.enter_context(tc.tile_pool(name="raw", bufs=1))
-        srt = ctx.enter_context(tc.tile_pool(name="srt", bufs=1))
+        srt = ctx.enter_context(tc.tile_pool(name="srt", bufs=3))
         keep = ctx.enter_context(tc.tile_pool(name="keep", bufs=1))
         stage = ctx.enter_context(tc.tile_pool(name="stage", bufs=3))
-        epi = ctx.enter_context(tc.tile_pool(name="epi", bufs=6))
+        prods = ctx.enter_context(tc.tile_pool(name="prods", bufs=2))
+        epi = ctx.enter_context(tc.tile_pool(name="epi", bufs=4))
         turned = ctx.enter_context(tc.psum_pool(name="turned", bufs=4))
         sums = ctx.enter_context(tc.psum_pool(name="sums", bufs=4))
 
@@ -92,29 +93,33 @@ def tile_attention_pa_kernel(tc, x, w, out_0, out_1):
         nc.vector.scalar_tensor_tensor(out=rest_neg[:], in0=rest[:], scalar=0.5, in1=rest[:], op0=ALU.is_gt,
                                        op1=ALU.subtract)
         sin_cos = const.tile([P, 2, TILES, FREQS], F32, name="sin_cos")
-        both = [const.tile([P, 2, 2, 2, DH], F32, name="both%d" % mp) for mp in range(2)]
+        table = [const.tile([P, 2, 2, 2, 2, FREQS], F32, name="table%d" % mp) for mp in range(2)]
 
         def take_sines():
             nc.scalar.activation(out=sin_cos[:].rearrange("p s m n -> p (s m n)"), in_=rest_neg[:], func=ACT.Sin,
                                  scale=-2.0 * PI)
 
-        def spread_tables(mp, eng):
+        def spread_tables(mp):
             for s in range(2):
                 for e in range(2):
                     sign = -1.0 if (s == 1 and e == 1) else 1.0
-                    eng.tensor_scalar(
-                        out=both[mp][:, s, :, :, :].rearrange("p m h (n e) -> p m h n e", e=2)[:, :, :, :, e],
+                    nc.vector.tensor_scalar(
+                        out=table[mp][:, s, :, :, e, :],
                         in0=sin_cos[:, 1 - s, 2 * mp:2 * mp + 2, :].unsqueeze(2).to_broadcast([P, 2, 2, FREQS]),
-                        scalar1=sign, scalar2=0.0, op0=ALU.mult, op1=ALU.add)
+                        scalar1=sign, scalar2=None, op0=ALU.mult)
 
         sorted_words = [None] * HEADS
 
-        def sort_words(h):
-            sorted_words[h] = srt.tile([P, K // 2], F32, name="sorted%d" % h)
-            nc.vector.tensor_copy(out=sorted_words[h][:].rearrange("p (g u j) -> p g u j", g=PASSES, u=2),
-                                  in_=w_raw[h][:].bitcast(F32).rearrange("p (g j u) -> p g u j", g=PASSES, u=2))
+        def sort_words(h, eng=None):
+            sorted_words[h] = srt.tile([P, K // 2], F32, name="sorted")
+            src = w_raw[h][:].bitcast(F32).rearrange("p (g j u) -> p g u j", g=PASSES, u=2)
+            dst = sorted_words[h][:].rearrange("p (g u j) -> p g u j", g=PASSES, u=2)
+            if eng is None:
+                nc.vector.tensor_copy(out=dst, in_=src)
+            else:
+                nc.scalar.copy(out=dst, in_=src)
 
-        def turn_two_passes(rows, gp, grouped, presorted=None):
+        def turn_two_passes(rows, gp, grouped, presorted=None, eng=None):
             words = rows[:].bitcast(F32)
             bank = turned.tile([P, BANK], F32, name="bank")
             for gl in range(2):
@@ -126,17 +131,20 @@ def tile_attention_pa_kernel(tc, x, w, out_0, out_1):
                     else:
                         nc.tensor.transpose(bank[:, s * P:(s + 1) * P],
                                             presorted[:, 256 * g + P * u:256 * g + P * (u + 1)], ident[:])
-            nc.scalar.copy(out=grouped, in_=bank[:].rearrange("p (g u r) -> p g r u", g=2, u=2))
+            if eng is None:
+                nc.scalar.copy(out=grouped, in_=bank[:].rearrange("p (g u r) -> p g r u", g=2, u=2))
+            else:
+                eng.tensor_copy(out=grouped, in_=bank[:].rearrange("p (g u r) -> p g r u", g=2, u=2))
 
         x_grouped = [None] * TILES
         x_codes = [keep.tile([P, PASSES * P], U32, name="x_codes%d" % m, align_bytes=64) for m in range(TILES)]
         x_scales = [keep.tile([P, PASSES * P], U8, name="x_scales%d" % m, align_bytes=64) for m in range(TILES)]
 
-        def turn_x(m):
-            x_grouped[m] = stage.tile([P, K], BF16, name="x_grouped", align_bytes=64)
+        def turn_x(m, gp, eng=None):
+            if x_grouped[m] is None:
+                x_grouped[m] = stage.tile([P, K], BF16, name="x_grouped", align_bytes=64)
             view = x_grouped[m][:].bitcast(F32).rearrange("p (g r u) -> p g r u", g=PASSES, u=2)
-            for gp in range(2):
-                turn_two_passes(x_raw[m], gp, view[:, 2 * gp:2 * gp + 2, :, :])
+            turn_two_passes(x_raw[m], gp, view[:, 2 * gp:2 * gp + 2, :, :], None, eng)
 
         def quantize_x(m):
             nc.vector.quantize_mx(out=x_codes[m][:].bitcast(FP8X4), scales=x_scales[m][:], in_=x_grouped[m][:])
@@ -145,11 +153,11 @@ def tile_attention_pa_kernel(tc, x, w, out_0, out_1):
         w_codes = [None] * PAIRS
         w_scales = [None] * PAIRS
 
-        def turn_w(hp, gp, hl):
+        def turn_w(hp, gp, hl, eng=None):
             if w_grouped[hp] is None:
                 w_grouped[hp] = stage.tile([P, 2 * K], BF16, name="w_grouped", align_bytes=64)
             view = w_grouped[hp][:].bitcast(F32).rearrange("p (g h d u) -> p g h d u", g=PASSES, h=2, u=2)
-            turn_two_passes(w_raw[2 * hp + hl], gp, view[:, 2 * gp:2 * gp + 2, hl, :, :], sorted_words[2 * hp + hl])
+            turn_two_passes(w_raw[2 * hp + hl], gp, view[:, 2 * gp:2 * gp + 2, hl, :, :], sorted_words[2 * hp + hl], eng)
 
         def turn_half(q):
             for hl in range(2):
@@ -166,11 +174,11 @@ def tile_attention_pa_kernel(tc, x, w, out_0, out_1):
         out0_rows = out_0.rearrange("h (p m) d -> p h m d", m=TILES)
         out1_rows = out_1.rearrange("h (p m) d -> p h m d", m=TILES)
         acc = [None] * UNITS
-        prod = [None] * UNITS
-        rot = [None] * PAIRS
-        row_amax = [None] * PAIRS
-        factor = [None] * PAIRS
-        codes = [None] * PAIRS
+        prod = {}
+        rot = {}
+        row_amax = {}
+        factor = {}
+        codes = {}
 
         def multiply(u):
             hp, mp = u // 2, u % 2
@@ -185,181 +193,166 @@ def tile_attention_pa_kernel(tc, x, w, out_0, out_1):
                                         rhs_scale=w_scales[hp][:, g * 2 * DH:(g + 1) * 2 * DH],
                                         start=(g == 0), stop=(g == PASSES - 1))
 
-        def products(u):
-            prod[u] = epi.tile([P, 2, BANK], F32, name="prod")
-            nc.vector.tensor_tensor(out=prod[u][:], in0=acc[u][:].unsqueeze(1).to_broadcast([P, 2, BANK]),
-                                    in1=both[u % 2][:].rearrange("p s m h d -> p s (m h d)"), op=ALU.mult)
+        def products(grp, k):
+            u0, n = grp
+            if k == 0:
+                prod[grp] = prods.tile([P, n, 2, BANK], F32, name="prod%d" % n)
+            u = u0 + k
+            nc.vector.tensor_tensor(out=prod[grp][:, k, :, :].rearrange("p s (q n e) -> p s q n e", q=4, e=2),
+                                    in0=acc[u][:].unsqueeze(1).to_broadcast([P, 2, BANK]).rearrange("p s (q n e) -> p s q n e", q=4, e=2),
+                                    in1=table[u % 2][:].rearrange("p s m h e n -> p s (m h) n e"), op=ALU.mult)
 
-        def add_and_store(u, eng):
-            hp, mp = u // 2, u % 2
-            if rot[hp] is None:
-                rot[hp] = epi.tile([P, 2, BANK], F32, name="rot")
-            eng.tensor_tensor(out=rot[hp][:, mp, :].rearrange("p (h m n e) -> p m h n e", h=2, m=2, e=2),
-                              in0=prod[u][:, 0, :].rearrange("p (m h n e) -> p m h n e", m=2, h=2, e=2),
-                              in1=prod[u][:, 1, :].rearrange("p (m h n e) -> p m h n e", m=2, h=2, e=2)[:, :, :, :, ::-1],
-                              op=ALU.add)
-            nc.sync.dma_start(out=out0_rows[:, 2 * hp:2 * hp + 2, 2 * mp:2 * mp + 2, :],
-                              in_=rot[hp][:, mp, :].rearrange("p (h m d) -> p h m d", h=2, m=2))
+        def store_rows(grp, dst, src):
+            u0, n = grp
+            hp, m0 = u0 // 2, 2 * (u0 % 2)
+            nc.sync.dma_start(out=dst[:, 2 * hp:2 * hp + 2, m0:m0 + 2 * n, :], in_=src.rearrange("p (h m d) -> p h m d", h=2, m=2 * n))
 
-        def take_row_amax(hp, lo, n):
-            if row_amax[hp] is None:
-                row_amax[hp] = epi.tile([P, 8], F32, name="row_amax")
-                factor[hp] = epi.tile([P, 8], F32, name="factor")
-            nc.vector.tensor_reduce(out=row_amax[hp][:, lo:lo + n],
-                                    in_=rot[hp][:].rearrange("p u (r d) -> p (u r) d", d=DH)[:, lo:lo + n, :],
+        def add_and_store(grp, eng=None):
+            u0, n = grp
+            rot[grp] = epi.tile([P, n * BANK], F32, name="rot%d" % n)
+            pairs = "p k (m h n e) -> p k m h n e"
+            (eng or nc.gpsimd).tensor_tensor(
+                out=rot[grp][:].rearrange("p (h k m n e) -> p k m h n e", h=2, k=n, m=2, e=2),
+                in0=prod[grp][:, :, 0, :].rearrange(pairs, m=2, h=2, e=2),
+                in1=prod[grp][:, :, 1, :].rearrange(pairs, m=2, h=2, e=2)[:, :, :, :, :, ::-1],
+                op=ALU.add)
+            store_rows(grp, out0_rows, rot[grp][:])
+
+        def add_one(grp, k, eng):
+            n = grp[1]
+            if k == 0:
+                rot[grp] = epi.tile([P, n * BANK], F32, name="rot%d" % n)
+            pairs = "p (m h n e) -> p m h n e"
+            eng.tensor_tensor(
+                out=rot[grp][:].rearrange("p (h k m n e) -> p k m h n e", h=2, k=n, m=2, e=2)[:, k, :, :, :, :],
+                in0=prod[grp][:, k, 0, :].rearrange(pairs, m=2, h=2, e=2),
+                in1=prod[grp][:, k, 1, :].rearrange(pairs, m=2, h=2, e=2)[:, :, :, :, ::-1],
+                op=ALU.add)
+
+        def take_row_amax(grp):
+            n = grp[1]
+            row_amax[grp] = epi.tile([P, 4 * n], F32, name="row_amax%d" % n)
+            nc.vector.tensor_reduce(out=row_amax[grp][:], in_=rot[grp][:].rearrange("p (r d) -> p r d", d=DH),
                                     axis=AX.X, op=ALU.max, apply_absolute_value=True)
 
-        def make_factor(hp, lo, n):
-            inverse = epi.tile([P, 8], F32, name="inverse")
-            nc.vector.reciprocal(out=inverse[:, lo:lo + n], in_=row_amax[hp][:, lo:lo + n])
-            nc.scalar.activation(out=factor[hp][:, lo:lo + n], in_=inverse[:, lo:lo + n], func=ACT.Copy, scale=448.0)
+        def invert(grp):
+            n = grp[1]
+            factor[grp] = [epi.tile([P, 4 * n], F32, name="inverse%d" % n), None]
+            nc.vector.reciprocal(out=factor[grp][0][:], in_=row_amax[grp][:])
 
-        def cast_rows(hp, lo, n, on_vector):
-            if codes[hp] is None:
-                codes[hp] = epi.tile([P, 2 * BANK], FP8, name="codes")
-            flat = rot[hp][:].rearrange("p u c -> p (u c)")
-            for r in range(lo, lo + n):
+        def make_factor(grp):
+            n = grp[1]
+            factor[grp][1] = epi.tile([P, 4 * n], F32, name="factor%d" % n)
+            nc.scalar.activation(out=factor[grp][1][:], in_=factor[grp][0][:], func=ACT.Copy, scale=448.0)
+
+        def cast_rows(grp, lo, hi, on_vector=False):
+            n = grp[1]
+            if grp not in codes:
+                codes[grp] = epi.tile([P, n * BANK], FP8, name="codes%d" % n)
+            for r in range(lo, hi):
                 cols = slice(r * DH, (r + 1) * DH)
-                if r >= lo + n - on_vector:
-                    nc.vector.tensor_scalar(out=codes[hp][:, cols], in0=flat[:, cols], scalar1=factor[hp][:, r:r + 1],
+                if on_vector:
+                    nc.vector.tensor_scalar(out=codes[grp][:, cols], in0=rot[grp][:, cols], scalar1=factor[grp][1][:, r:r + 1],
                                             scalar2=None, op0=ALU.mult, saturate=False)
                 else:
-                    nc.scalar.activation(out=codes[hp][:, cols], in_=flat[:, cols], func=ACT.Identity,
-                                         scale=factor[hp][:, r:r + 1], bias=zeros[:, 0:1], saturate=False)
+                    nc.scalar.activation(out=codes[grp][:, cols], in_=rot[grp][:, cols], func=ACT.Identity,
+                                         scale=factor[grp][1][:, r:r + 1], bias=zeros[:, 0:1], saturate=False)
 
-        def store_codes(hp, mp, n):
-            for q in range(mp, mp + n):
-                nc.sync.dma_start(out=out1_rows[:, 2 * hp:2 * hp + 2, 2 * q:2 * q + 2, :],
-                                  in_=codes[hp][:, q * BANK:(q + 1) * BANK].bitcast(U8).rearrange("p (h m d) -> p h m d", h=2, m=2))
+        def store_codes(grp):
+            store_rows(grp, out1_rows, codes[grp][:].bitcast(U8))
 
-        turn_x(0)
-        turn_x(1)
+        V = nc.vector
+
+        def turn_head(h, engs=(None, None)):
+            for gp in range(2):
+                turn_w(h // 2, gp, h % 2, engs[gp])
+
+        G = [(2 * v, 2) for v in range(PAIRS)]
+        turn_x(0, 0)
+        turn_x(0, 1)
         quantize_x(0)
-        take_sines()
+        turn_x(1, 0)
+        turn_x(1, 1, V)
         quantize_x(1)
-        turn_w(0, 0, 0)
-        turn_w(0, 1, 0)
-        turn_w(0, 0, 1)
-        turn_w(0, 1, 1)
-        spread_tables(0, nc.vector)
-        quantize_passes(0, 0, 2)
-        quantize_passes(0, 2, 2)
-        turn_x(2)
+        take_sines()
+        spread_tables(0)
+        turn_head(0)
+        turn_head(1)
+        spread_tables(1)
+        quantize_passes(0, 0, 4)
+        turn_x(2, 0)
+        turn_x(2, 1)
+        turn_x(3, 0)
+        turn_x(3, 1)
         quantize_x(2)
-        turn_x(3)
         multiply(0)
+        sort_words(2)
+        turn_head(2)
         quantize_x(3)
-        spread_tables(1, nc.gpsimd)
-        turn_half(2)
-        products(0)
-        add_and_store(0, nc.gpsimd)
+        turn_head(3)
+        multiply(1)
+        products(G[0], 0)
         sort_words(4)
         sort_words(5)
-        quantize_passes(1, 0, 2)
-        turn_half(3)
-        multiply(1)
-        turn_half(4)
-        turn_half(5)
-        quantize_passes(1, 2, 2)
+        add_one(G[0], 0, V)
+        sort_words(6, nc.scalar)
+        turn_head(4)
+        turn_head(5)
+        sort_words(7, nc.scalar)
+        quantize_passes(1, 0, 4)
+        products(G[0], 1)
+        add_one(G[0], 1, V)
+        store_rows(G[0], out0_rows, rot[G[0]][:])
         multiply(2)
         multiply(3)
-        products(1)
-        add_and_store(1, nc.gpsimd)
-        sort_words(6)
-        sort_words(7)
         quantize_passes(2, 0, 4)
-        turn_half(6)
-        turn_half(7)
+        turn_head(6)
+        turn_head(7)
         multiply(4)
         multiply(5)
-        products(2)
-        add_and_store(2, nc.gpsimd)
-        products(3)
-        add_and_store(3, nc.gpsimd)
-        take_row_amax(0, 0, 8)
-        quantize_passes(3, 0, 4)
-        turn_half(8)
-        turn_half(9)
-        multiply(6)
-        multiply(7)
-        products(4)
-        add_and_store(4, nc.gpsimd)
-        make_factor(0, 0, 8)
-        cast_rows(0, 0, 8, 0)
-        store_codes(0, 0, 2)
-        products(5)
-        add_and_store(5, nc.gpsimd)
-        take_row_amax(1, 0, 8)
-        quantize_passes(4, 0, 4)
-        turn_half(10)
-        turn_half(11)
-        multiply(8)
-        multiply(9)
-        products(6)
-        add_and_store(6, nc.gpsimd)
-        make_factor(1, 0, 8)
-        cast_rows(1, 0, 8, 0)
-        store_codes(1, 0, 2)
-        products(7)
-        add_and_store(7, nc.gpsimd)
-        take_row_amax(2, 0, 8)
-        quantize_passes(5, 0, 4)
-        turn_half(12)
-        turn_half(13)
-        multiply(10)
-        multiply(11)
-        products(8)
-        add_and_store(8, nc.gpsimd)
-        make_factor(2, 0, 8)
-        cast_rows(2, 0, 8, 0)
-        store_codes(2, 0, 2)
-        products(9)
-        add_and_store(9, nc.gpsimd)
-        take_row_amax(3, 0, 8)
-        quantize_passes(6, 0, 4)
-        turn_half(14)
-        turn_half(15)
-        multiply(12)
-        multiply(13)
-        products(10)
-        add_and_store(10, nc.gpsimd)
-        make_factor(3, 0, 8)
-        cast_rows(3, 0, 8, 0)
-        store_codes(3, 0, 2)
-        products(11)
-        add_and_store(11, nc.gpsimd)
-        take_row_amax(4, 0, 8)
-        quantize_passes(7, 0, 4)
-        multiply(14)
-        multiply(15)
-        products(12)
-        add_and_store(12, nc.gpsimd)
-        make_factor(4, 0, 8)
-        cast_rows(4, 0, 8, 0)
-        store_codes(4, 0, 2)
-        products(13)
-        add_and_store(13, nc.gpsimd)
-        take_row_amax(5, 0, 8)
-        products(14)
-        add_and_store(14, nc.gpsimd)
-        make_factor(5, 0, 8)
-        cast_rows(5, 0, 8, 0)
-        store_codes(5, 0, 2)
-        take_row_amax(6, 0, 4)
-        products(15)
-        add_and_store(15, nc.gpsimd)
-        make_factor(6, 0, 4)
-        cast_rows(6, 0, 4, 0)
-        store_codes(6, 0, 1)
-        take_row_amax(6, 4, 4)
-        take_row_amax(7, 0, 4)
-        make_factor(6, 4, 4)
-        cast_rows(6, 4, 4, 0)
-        store_codes(6, 1, 1)
-        make_factor(7, 0, 4)
-        cast_rows(7, 0, 4, 0)
-        store_codes(7, 0, 1)
-        take_row_amax(7, 4, 4)
-        make_factor(7, 4, 4)
-        cast_rows(7, 4, 4, 2)
-        store_codes(7, 1, 1)
+        DR = 6
+        for v in range(1, DR):
+            products(G[v], 0)
+            if v >= 2:
+                invert(G[v - 2])
+                make_factor(G[v - 2])
+                cast_rows(G[v - 2], 0, 8)
+                store_codes(G[v - 2])
+            products(G[v], 1)
+            quantize_passes(v + 2, 0, 4)
+            add_and_store(G[v])
+            take_row_amax(G[v - 1])
+            if v + 3 < PAIRS:
+                turn_half(2 * v + 6)
+                turn_half(2 * v + 7)
+            multiply(2 * v + 4)
+            multiply(2 * v + 5)
+        A, B, C, E = (12, 1), (13, 1), (14, 1), (15, 1)
+
+        def finish(grp, on_vector=0):
+            invert(grp)
+            make_factor(grp)
+            cast_rows(grp, 0, 4 * grp[1] - on_vector)
+            if on_vector:
+                cast_rows(grp, 4 * grp[1] - on_vector, 4 * grp[1], True)
+            store_codes(grp)
+
+        products(A, 0)
+        add_and_store(A)
+        finish(G[4])
+        products(B, 0)
+        add_and_store(B)
+        take_row_amax(G[5])
+        products(C, 0)
+        add_and_store(C)
+        finish(G[5])
+        take_row_amax(A)
+        products(E, 0)
+        add_and_store(E)
+        finish(A)
+        take_row_amax(B)
+        take_row_amax(C)
+        finish(B)
+        finish(C)
+        take_row_amax(E)
+        finish(E, 2)

@@ -218,6 +218,11 @@ def tile_attention_pa_kernel(tc, x, w, out_0, out_1):
                 op=ALU.add)
             store_rows(grp, out0_rows, rot[grp][:])
 
+        gate = const.tile([P, PAIRS], U32, name="gate")
+
+        def gpsimd_waits_for_codes(hp):
+            nc.gpsimd.tensor_copy(out=gate[:, hp:hp + 1], in_=w_codes[hp][:, 0:1])
+
         def add_one(grp, k, eng):
             n = grp[1]
             if k == 0:
@@ -295,17 +300,18 @@ def tile_attention_pa_kernel(tc, x, w, out_0, out_1):
         sort_words(4)
         sort_words(5)
         add_one(G[0], 0, V)
-        sort_words(6, nc.scalar)
         turn_head(4)
         turn_head(5)
         sort_words(7, nc.scalar)
         quantize_passes(1, 0, 4)
         products(G[0], 1)
-        add_one(G[0], 1, V)
-        store_rows(G[0], out0_rows, rot[G[0]][:])
+        sort_words(6)
         multiply(2)
         multiply(3)
         quantize_passes(2, 0, 4)
+        gpsimd_waits_for_codes(2)
+        add_one(G[0], 1, nc.gpsimd)
+        store_rows(G[0], out0_rows, rot[G[0]][:])
         turn_head(6)
         turn_head(7)
         multiply(4)
@@ -313,15 +319,25 @@ def tile_attention_pa_kernel(tc, x, w, out_0, out_1):
         DR = 6
         for v in range(1, DR):
             products(G[v], 0)
+            if v == 1:
+                add_one(G[v], 0, nc.gpsimd)
             if v >= 2:
                 invert(G[v - 2])
                 make_factor(G[v - 2])
                 cast_rows(G[v - 2], 0, 8)
                 store_codes(G[v - 2])
             products(G[v], 1)
+            if v == 1:
+                take_row_amax(G[0])
             quantize_passes(v + 2, 0, 4)
-            add_and_store(G[v])
-            take_row_amax(G[v - 1])
+            gpsimd_waits_for_codes(v + 2)
+            if v == 1:
+                add_one(G[v], 1, nc.gpsimd)
+                store_rows(G[v], out0_rows, rot[G[v]][:])
+            else:
+                add_and_store(G[v])
+            if v > 1:
+                take_row_amax(G[v - 1])
             if v + 3 < PAIRS:
                 turn_half(2 * v + 6)
                 turn_half(2 * v + 7)

@@ -93,20 +93,21 @@ def tile_attention_pa_kernel(tc, x, w, out_0, out_1):
         nc.vector.scalar_tensor_tensor(out=rest_neg[:], in0=rest[:], scalar=0.5, in1=rest[:], op0=ALU.is_gt,
                                        op1=ALU.subtract)
         sin_cos = const.tile([P, 2, TILES, FREQS], F32, name="sin_cos")
-        table = [const.tile([P, 2, 2, 2, 2, FREQS], F32, name="table%d" % mp) for mp in range(2)]
+        table = [const.tile([P, 2, 2, FREQS, 2], F32, name="table%d" % mp) for mp in range(2)]
+        sign = const.tile([P, 2, 2], F32, name="sign")
+        nc.vector.memset(sign[:], 1.0)
+        nc.vector.memset(sign[:, 0, 1:2], -1.0)
 
         def take_sines():
             nc.scalar.activation(out=sin_cos[:].rearrange("p s m n -> p (s m n)"), in_=rest_neg[:], func=ACT.Sin,
                                  scale=-2.0 * PI)
 
         def spread_tables(mp):
-            for s in range(2):
-                for e in range(2):
-                    sign = -1.0 if (s == 1 and e == 1) else 1.0
-                    nc.vector.tensor_scalar(
-                        out=table[mp][:, s, :, :, e, :],
-                        in0=sin_cos[:, 1 - s, 2 * mp:2 * mp + 2, :].unsqueeze(2).to_broadcast([P, 2, 2, FREQS]),
-                        scalar1=sign, scalar2=None, op0=ALU.mult)
+            shape = [P, 2, 2 * FREQS, 2]
+            nc.vector.tensor_tensor(
+                out=table[mp][:].rearrange("p s m n e -> p s (m n) e"),
+                in0=sin_cos[:, :, 2 * mp:2 * mp + 2, :].rearrange("p s m n -> p s (m n)").unsqueeze(3).to_broadcast(shape),
+                in1=sign[:].unsqueeze(2).to_broadcast(shape), op=ALU.mult)
 
         sorted_words = [None] * HEADS
 
@@ -198,9 +199,10 @@ def tile_attention_pa_kernel(tc, x, w, out_0, out_1):
             if k == 0:
                 prod[grp] = prods.tile([P, n, 2, BANK], F32, name="prod%d" % n)
             u = u0 + k
-            nc.vector.tensor_tensor(out=prod[grp][:, k, :, :].rearrange("p s (q n e) -> p s q n e", q=4, e=2),
-                                    in0=acc[u][:].unsqueeze(1).to_broadcast([P, 2, BANK]).rearrange("p s (q n e) -> p s q n e", q=4, e=2),
-                                    in1=table[u % 2][:].rearrange("p s m h e n -> p s (m h) n e"), op=ALU.mult)
+            nc.vector.tensor_tensor(out=prod[grp][:, k, :, :].rearrange("p s (m h d) -> p s m h d", m=2, h=2),
+                                    in0=acc[u][:].unsqueeze(1).to_broadcast([P, 2, BANK]).rearrange("p s (m h d) -> p s m h d", m=2, h=2),
+                                    in1=table[u % 2][:].rearrange("p s m n e -> p s m (n e)").unsqueeze(3).to_broadcast([P, 2, 2, 2, DH]),
+                                    op=ALU.mult)
 
         def store_rows(grp, dst, src):
             u0, n = grp
@@ -213,8 +215,8 @@ def tile_attention_pa_kernel(tc, x, w, out_0, out_1):
             pairs = "p k (m h n e) -> p k m h n e"
             (eng or nc.gpsimd).tensor_tensor(
                 out=rot[grp][:].rearrange("p (h k m n e) -> p k m h n e", h=2, k=n, m=2, e=2),
-                in0=prod[grp][:, :, 0, :].rearrange(pairs, m=2, h=2, e=2),
-                in1=prod[grp][:, :, 1, :].rearrange(pairs, m=2, h=2, e=2)[:, :, :, :, :, ::-1],
+                in0=prod[grp][:, :, 1, :].rearrange(pairs, m=2, h=2, e=2),
+                in1=prod[grp][:, :, 0, :].rearrange(pairs, m=2, h=2, e=2)[:, :, :, :, :, ::-1],
                 op=ALU.add)
             store_rows(grp, out0_rows, rot[grp][:])
 
@@ -230,8 +232,8 @@ def tile_attention_pa_kernel(tc, x, w, out_0, out_1):
             pairs = "p (m h n e) -> p m h n e"
             eng.tensor_tensor(
                 out=rot[grp][:].rearrange("p (h k m n e) -> p k m h n e", h=2, k=n, m=2, e=2)[:, k, :, :, :, :],
-                in0=prod[grp][:, k, 0, :].rearrange(pairs, m=2, h=2, e=2),
-                in1=prod[grp][:, k, 1, :].rearrange(pairs, m=2, h=2, e=2)[:, :, :, :, ::-1],
+                in0=prod[grp][:, k, 1, :].rearrange(pairs, m=2, h=2, e=2),
+                in1=prod[grp][:, k, 0, :].rearrange(pairs, m=2, h=2, e=2)[:, :, :, :, ::-1],
                 op=ALU.add)
 
         def take_row_amax(grp):

@@ -321,25 +321,18 @@ def tile_attention_pa_kernel(tc, x, w, out_0, out_1):
         DR = 6
         for v in range(1, DR):
             products(G[v], 0)
-            if v == 1:
-                add_one(G[v], 0, nc.gpsimd)
+            add_one(G[v], 0, nc.gpsimd)
             if v >= 2:
                 invert(G[v - 2])
                 make_factor(G[v - 2])
                 cast_rows(G[v - 2], 0, 8)
                 store_codes(G[v - 2])
             products(G[v], 1)
-            if v == 1:
-                take_row_amax(G[0])
+            take_row_amax(G[v - 1])
             quantize_passes(v + 2, 0, 4)
             gpsimd_waits_for_codes(v + 2)
-            if v == 1:
-                add_one(G[v], 1, nc.gpsimd)
-                store_rows(G[v], out0_rows, rot[G[v]][:])
-            else:
-                add_and_store(G[v])
-            if v > 1:
-                take_row_amax(G[v - 1])
+            add_one(G[v], 1, nc.gpsimd)
+            store_rows(G[v], out0_rows, rot[G[v]][:])
             if v + 3 < PAIRS:
                 turn_half(2 * v + 6)
                 turn_half(2 * v + 7)

@@ -31,6 +31,7 @@ BANK = 512
 def tile_attention_pa_kernel(tc, x, w, out_0, out_1):
     nc = tc.nc
     with ExitStack() as ctx:
+        PRM = {2: "V", 4: "V", 5: "V", 6: "V", 7: "S", 9: "S", 12: "S", "fence": 1, "gpos": 1, "gu": (), "o3": 0, "o2": 0, "addV": 1, "split": 9, "redfirst": 9, "mm0": 1, "p0": 1, "spG": 0, "vc": ["x1b"], "deep": 9}
         ctx.enter_context(tc.manual_schedule())
         const = ctx.enter_context(tc.tile_pool(name="const", bufs=1))
         raw = ctx.enter_context(tc.tile_pool(name="raw", bufs=1))
@@ -104,7 +105,7 @@ def tile_attention_pa_kernel(tc, x, w, out_0, out_1):
 
         def spread_tables(mp):
             shape = [P, 2, 2 * FREQS, 2]
-            nc.vector.tensor_tensor(
+            (nc.gpsimd if PRM["spG"] else nc.vector).tensor_tensor(
                 out=table[mp][:].rearrange("p s m n e -> p s (m n) e"),
                 in0=sin_cos[:, :, 2 * mp:2 * mp + 2, :].rearrange("p s m n -> p s (m n)").unsqueeze(3).to_broadcast(shape),
                 in1=sign[:].unsqueeze(2).to_broadcast(shape), op=ALU.mult)
@@ -113,12 +114,16 @@ def tile_attention_pa_kernel(tc, x, w, out_0, out_1):
 
         def sort_words(h, eng=None):
             sorted_words[h] = srt.tile([P, K // 2], F32, name="sorted")
-            src = w_raw[h][:].bitcast(F32).rearrange("p (g j u) -> p g u j", g=PASSES, u=2)
-            dst = sorted_words[h][:].rearrange("p (g u j) -> p g u j", g=PASSES, u=2)
+            src = w_raw[h][:].bitcast(F32).rearrange("p (w u) -> p u w", u=2)
+            dst = sorted_words[h][:].rearrange("p (u w) -> p u w", u=2)
             if eng is None:
                 nc.vector.tensor_copy(out=dst, in_=src)
-            else:
+            elif eng is nc.scalar:
                 nc.scalar.copy(out=dst, in_=src)
+            else:
+                nc.gpsimd.tensor_scalar(out=sorted_words[h][:].bitcast(BF16).rearrange("p (u w e) -> p u w e", u=2, e=2),
+                                        in0=w_raw[h][:].rearrange("p (w u e) -> p u w e", u=2, e=2),
+                                        scalar1=1.0, scalar2=0.0, op0=ALU.mult, op1=ALU.add)
 
         def turn_two_passes(rows, gp, grouped, presorted=None, eng=None):
             words = rows[:].bitcast(F32)
@@ -131,7 +136,7 @@ def tile_attention_pa_kernel(tc, x, w, out_0, out_1):
                         nc.tensor.transpose(bank[:, s * P:(s + 1) * P], words[:, 256 * g + u:256 * (g + 1):2], ident[:])
                     else:
                         nc.tensor.transpose(bank[:, s * P:(s + 1) * P],
-                                            presorted[:, 256 * g + P * u:256 * g + P * (u + 1)], ident[:])
+                                            presorted[:, 512 * u + P * g:512 * u + P * (g + 1)], ident[:])
             if eng is None:
                 nc.scalar.copy(out=grouped, in_=bank[:].rearrange("p (g u r) -> p g r u", g=2, u=2))
             else:
@@ -204,6 +209,17 @@ def tile_attention_pa_kernel(tc, x, w, out_0, out_1):
                                     in1=table[u % 2][:].rearrange("p s m n e -> p s m (n e)").unsqueeze(3).to_broadcast([P, 2, 2, 2, DH]),
                                     op=ALU.mult)
 
+        def products_gpsimd(grp, k):
+            u = grp[0] + k
+            if k == 0:
+                prod[grp] = prods.tile([P, grp[1], 2, BANK], F32, name="prod%d" % grp[1])
+            held = epi.tile([P, BANK], F32, name="held")
+            nc.scalar.copy(out=held[:], in_=acc[u][:])
+            nc.gpsimd.tensor_tensor(out=prod[grp][:, k, :, :].rearrange("p s (m h d) -> p s m h d", m=2, h=2),
+                                    in0=held[:].unsqueeze(1).to_broadcast([P, 2, BANK]).rearrange("p s (m h d) -> p s m h d", m=2, h=2),
+                                    in1=table[u % 2][:].rearrange("p s m n e -> p s m (n e)").unsqueeze(3).to_broadcast([P, 2, 2, 2, DH]),
+                                    op=ALU.mult)
+
         def store_rows(grp, dst, src):
             u0, n = grp
             hp, m0 = u0 // 2, 2 * (u0 % 2)
@@ -269,75 +285,131 @@ def tile_attention_pa_kernel(tc, x, w, out_0, out_1):
             store_rows(grp, out1_rows, codes[grp][:].bitcast(U8))
 
         V = nc.vector
+        ENG = {"V": None, "V3": None, "S": nc.scalar, "G": nc.gpsimd}
+
+        def at(h, e):
+            if PRM.get(h) == e:
+                sort_words(h, ENG[e])
 
         def turn_head(h, engs=(None, None)):
             for gp in range(2):
                 turn_w(h // 2, gp, h % 2, engs[gp])
 
         G = [(2 * v, 2) for v in range(PAIRS)]
-        turn_x(0, 0)
-        turn_x(0, 1)
+        def on(name):
+            return V if name in PRM["vc"] else None
+
+        turn_x(0, 0, on("x0a"))
+        turn_x(0, 1, on("x0b"))
         quantize_x(0)
-        turn_x(1, 0)
-        turn_x(1, 1, V)
+        turn_x(1, 0, on("x1a"))
+        turn_x(1, 1, on("x1b"))
         quantize_x(1)
         take_sines()
         spread_tables(0)
-        turn_head(0)
-        turn_head(1)
+        turn_head(0, (on("w0a"), on("w0b")))
+        turn_head(1, (on("w1a"), on("w1b")))
         spread_tables(1)
         quantize_passes(0, 0, 4)
-        turn_x(2, 0)
-        turn_x(2, 1)
-        turn_x(3, 0)
-        turn_x(3, 1)
+        turn_x(2, 0, on("x2a"))
+        turn_x(2, 1, on("x2b"))
+        if PRM["mm0"] == 0:
+            multiply(0)
+        turn_x(3, 0, on("x3a"))
+        turn_x(3, 1, on("x3b"))
         quantize_x(2)
-        multiply(0)
-        sort_words(2)
+        if PRM["mm0"] == 1:
+            multiply(0)
+        at(2, "V")
         turn_head(2)
+        if PRM["p0"] == 0:
+            products(G[0], 0)
+        at(3, "S")
+        at(3, "V3")
         quantize_x(3)
+        at(3, "V")
         turn_head(3)
         multiply(1)
-        products(G[0], 0)
-        sort_words(4)
-        sort_words(5)
-        add_one(G[0], 0, V)
-        turn_head(4)
-        turn_head(5)
-        sort_words(7, nc.scalar)
+        at(4, "G")
+        at(5, "G")
+        at(6, "G")
+        at(7, "G")
+        at(8, "G")
+        at(9, "G")
+        if PRM["p0"] == 1:
+            products(G[0], 0)
+        at(4, "V")
+        at(5, "V")
+        if PRM["addV"] >= 1:
+            add_one(G[0], 0, V)
+        else:
+            add_one(G[0], 0, nc.gpsimd)
+        turn_head(5 if PRM["o2"] else 4)
+        at(6, "S")
+        turn_head(4 if PRM["o2"] else 5)
+        at(7, "S")
         quantize_passes(1, 0, 4)
         products(G[0], 1)
-        sort_words(6)
+        at(6, "V")
+        at(7, "V")
+        if PRM["addV"] >= 2:
+            add_one(G[0], 1, V)
         multiply(2)
         multiply(3)
         quantize_passes(2, 0, 4)
-        gpsimd_waits_for_codes(2)
-        add_one(G[0], 1, nc.gpsimd)
+        if PRM["fence"]:
+            gpsimd_waits_for_codes(2)
+        if PRM["addV"] < 2:
+            add_one(G[0], 1, nc.gpsimd)
         store_rows(G[0], out0_rows, rot[G[0]][:])
-        turn_head(6)
-        turn_head(7)
+        turn_head(7 if PRM["o3"] else 6)
+        turn_head(6 if PRM["o3"] else 7)
         multiply(4)
         multiply(5)
+        at(8, "S")
+        at(9, "S")
         DR = 6
+        turned_pairs = 4
+
+        def turn_pair(hp):
+            turn_half(2 * hp)
+            turn_half(2 * hp + 1)
+
         for v in range(1, DR):
-            products(G[v], 0)
-            add_one(G[v], 0, nc.gpsimd)
+            if v not in PRM["gu"]:
+                products(G[v], 0)
+            if v + 1 in PRM["gu"] and PRM["gpos"] == 0:
+                products_gpsimd(G[v + 1], 0)
+            if v <= PRM["split"]:
+                add_one(G[v], 0, nc.gpsimd)
             if v >= 2:
                 invert(G[v - 2])
                 make_factor(G[v - 2])
                 cast_rows(G[v - 2], 0, 8)
                 store_codes(G[v - 2])
             products(G[v], 1)
-            take_row_amax(G[v - 1])
+            if v <= PRM["redfirst"]:
+                take_row_amax(G[v - 1])
             quantize_passes(v + 2, 0, 4)
-            gpsimd_waits_for_codes(v + 2)
-            add_one(G[v], 1, nc.gpsimd)
-            store_rows(G[v], out0_rows, rot[G[v]][:])
-            if v + 3 < PAIRS:
-                turn_half(2 * v + 6)
-                turn_half(2 * v + 7)
+            if PRM["fence"]:
+                gpsimd_waits_for_codes(v + 2)
+            if v <= PRM["split"]:
+                add_one(G[v], 1, nc.gpsimd)
+                store_rows(G[v], out0_rows, rot[G[v]][:])
+            else:
+                add_and_store(G[v])
+            if v + 1 in PRM["gu"] and PRM["gpos"] == 1:
+                products_gpsimd(G[v + 1], 0)
+            if v > PRM["redfirst"]:
+                take_row_amax(G[v - 1])
+            while turned_pairs < PAIRS and turned_pairs <= (v + 4 if v >= PRM["deep"] else v + 3):
+                turn_pair(turned_pairs)
+                turned_pairs += 1
             multiply(2 * v + 4)
             multiply(2 * v + 5)
+            for h in (2 * v + 8, 2 * v + 9):
+                at(h, "S")
+                at(h, "G")
         A, B, C, E = (12, 1), (13, 1), (14, 1), (15, 1)
 
         def finish(grp, on_vector=0):

@@ -31,7 +31,7 @@ BANK = 512
 def tile_attention_pa_kernel(tc, x, w, out_0, out_1):
     nc = tc.nc
     with ExitStack() as ctx:
-        PRM = {2: "V", 4: "V", 5: "V", 6: "V", 7: "S", 9: "S", 12: "S", "fence": 1, "gpos": 1, "gu": (), "o3": 0, "o2": 0, "addV": 1, "split": 9, "redfirst": 9, "mm0": 1, "p0": 1, "spG": 0, "vc": ["x1b"], "deep": 9}
+        PRM = {2: "V", 3: "V", 4: "V", 5: "V", 6: "V", 7: "S", 9: "S", 11: "S", 15: "S", "fence": 1, "gpos": 1, "gu": (), "o3": 0, "o2": 0, "addV": 1, "split": 9, "redfirst": 9, "mm0": 1, "p0": 1, "spG": 0, "vc": ["x1b"], "deep": 9}
         ctx.enter_context(tc.manual_schedule())
         const = ctx.enter_context(tc.tile_pool(name="const", bufs=1))
         raw = ctx.enter_context(tc.tile_pool(name="raw", bufs=1))
@@ -436,6 +436,14 @@ def tile_attention_pa_kernel(tc, x, w, out_0, out_1):
         take_row_amax(B)
         take_row_amax(C)
         finish(B)
-        finish(C)
+        invert(C)
+        make_factor(C)
+        cast_rows(C, 0, 2)
         take_row_amax(E)
-        finish(E, 2)
+        invert(E)
+        cast_rows(C, 2, 4, True)
+        store_codes(C)
+        make_factor(E)
+        cast_rows(E, 0, 2)
+        cast_rows(E, 2, 4, True)
+        store_codes(E)

@@ -438,12 +438,11 @@ def tile_attention_pa_kernel(tc, x, w, out_0, out_1):
         finish(B)
         invert(C)
         make_factor(C)
-        cast_rows(C, 0, 2)
         take_row_amax(E)
         invert(E)
-        cast_rows(C, 2, 4, True)
-        store_codes(C)
         make_factor(E)
+        cast_rows(C, 0, 4, True)
+        store_codes(C)
         cast_rows(E, 0, 2)
         cast_rows(E, 2, 4, True)
         store_codes(E)

@@ -54,20 +54,22 @@ def tile_attention_pa_kernel(tc, x, w, out_0, out_1):
         x_raw = [raw.tile([P, K], BF16, name="x%d" % m) for m in range(TILES)]
         w_raw = [raw.tile([P, K], BF16, name="w%d" % h) for h in range(HEADS)]
 
-        def load_x(m):
-            nc.sync.dma_start(out=x_raw[m][:], in_=x_tiles[m])
+        def load(dst, src, parts):
+            width = K // parts
+            for c in range(parts):
+                nc.sync.dma_start(out=dst[:, c * width:(c + 1) * width], in_=src[:, c * width:(c + 1) * width])
 
-        def load_w(h):
-            nc.sync.dma_start(out=w_raw[h][:], in_=w[h * P:(h + 1) * P, :])
+        def w_rows(h):
+            return w[h * P:(h + 1) * P, :]
 
-        load_x(0)
-        load_x(1)
-        load_w(0)
-        load_w(1)
-        load_x(2)
-        load_x(3)
+        load(x_raw[0], x_tiles[0], 2)
+        load(x_raw[1], x_tiles[1], 2)
+        load(w_raw[0], w_rows(0), 2)
+        load(w_raw[1], w_rows(1), 2)
+        load(x_raw[2], x_tiles[2], 2)
+        load(x_raw[3], x_tiles[3], 2)
         for h in range(2, HEADS):
-            load_w(h)
+            load(w_raw[h], w_rows(h), 1)
 
         freq = const.tile([P, FREQS], F32, name="freq")
         nc.vector.memset(freq[:, 0:1], 1.0)

@@ -312,7 +312,8 @@ def tile_attention_pa_kernel(tc, x, w, out_0, out_1):
         turn_head(0, (on("w0a"), on("w0b")))
         turn_head(1, (on("w1a"), on("w1b")))
         spread_tables(1)
-        quantize_passes(0, 0, 4)
+        quantize_passes(0, 0, 2)
+        quantize_passes(0, 2, 2)
         turn_x(2, 0, on("x2a"))
         turn_x(2, 1, on("x2b"))
         if PRM["mm0"] == 0:

from contextlib import ExitStack

import concourse.mybir as mybir
from concourse.masks import make_identity

TOKENS, K, HEADS, DH = 512, 2048, 16, 128
ROPE_BASE = 10000.0
PI = 3.141592653589793
FLOPS = 2 * TOKENS * K * HEADS * DH

F32 = mybir.dt.float32
BF16 = mybir.dt.bfloat16
U32 = mybir.dt.uint32
I32 = mybir.dt.int32
U8 = mybir.dt.uint8
FP8X4 = mybir.dt.float8_e4m3fn_x4
FP8 = mybir.dt.float8_e4m3fn
ALU = mybir.AluOpType
ACT = mybir.ActivationFunctionType
AX = mybir.AxisListType

P = 128
PASSES = K // (4 * P)
TILES = TOKENS // P
PAIRS = HEADS // 2
UNITS = 2 * PAIRS
FREQS = DH // 2
BANK = 512


def tile_attention_pa_kernel(tc, x, w, out_0, out_1):
    nc = tc.nc
    with ExitStack() as ctx:
        PRM = {2: "V", 3: "V", 4: "V", 5: "V", 6: "V", 7: "S", 9: "S", 11: "S", 15: "S", "fence": 1, "gpos": 1, "gu": (), "o3": 0, "o2": 0, "addV": 1, "split": 9, "redfirst": 9, "mm0": 1, "p0": 1, "spG": 0, "vc": ["x1b"], "deep": 9}
        ctx.enter_context(tc.manual_schedule())
        const = ctx.enter_context(tc.tile_pool(name="const", bufs=1))
        raw = ctx.enter_context(tc.tile_pool(name="raw", bufs=1))
        srt = ctx.enter_context(tc.tile_pool(name="srt", bufs=3))
        keep = ctx.enter_context(tc.tile_pool(name="keep", bufs=1))
        stage = ctx.enter_context(tc.tile_pool(name="stage", bufs=3))
        prods = ctx.enter_context(tc.tile_pool(name="prods", bufs=2))
        epi = ctx.enter_context(tc.tile_pool(name="epi", bufs=4))
        turned = ctx.enter_context(tc.psum_pool(name="turned", bufs=4))
        sums = ctx.enter_context(tc.psum_pool(name="sums", bufs=4))

        ident = const.tile([P, P], F32, name="ident")
        make_identity(nc, ident[:])
        zeros = const.tile([P, 1], F32, name="zeros")
        nc.vector.memset(zeros[:], 0.0)
        first_sin = const.tile([P, 1], F32, name="first_sin")
        nc.scalar.activation(out=first_sin[:], in_=zeros[:], func=ACT.Sin)

        x_tiles = x.rearrange("(p m) k -> m p k", m=TILES)
        x_raw = [raw.tile([P, K], BF16, name="x%d" % m) for m in range(TILES)]
        w_raw = [raw.tile([P, K], BF16, name="w%d" % h) for h in range(HEADS)]

        def load(dst, src, parts):
            width = K // parts
            for c in range(parts):
                nc.sync.dma_start(out=dst[:, c * width:(c + 1) * width], in_=src[:, c * width:(c + 1) * width])

        def w_rows(h):
            return w[h * P:(h + 1) * P, :]

        load(x_raw[0], x_tiles[0], 2)
        load(x_raw[1], x_tiles[1], 2)
        load(w_raw[0], w_rows(0), 2)
        load(w_raw[1], w_rows(1), 2)
        load(x_raw[2], x_tiles[2], 2)
        load(x_raw[3], x_tiles[3], 2)
        for h in range(2, HEADS):
            load(w_raw[h], w_rows(h), 1)

        freq = const.tile([P, FREQS], F32, name="freq")
        nc.vector.memset(freq[:, 0:1], 1.0)
        for n in (1, 2, 4, 8, 16, 32):
            nc.vector.tensor_scalar(out=freq[:, n:2 * n], in0=freq[:, 0:n], scalar1=ROPE_BASE ** (-n / float(FREQS)),
                                    scalar2=None, op0=ALU.mult)
        token_i = const.tile([P, TILES], I32, name="token_i")
        nc.gpsimd.iota(token_i[:], pattern=[[1, TILES]], base=0, channel_multiplier=TILES)
        token = const.tile([P, TILES], F32, name="token")
        nc.vector.tensor_copy(out=token[:], in_=token_i[:])
        turns = const.tile([P, 2, TILES, FREQS], F32, name="turns")
        for m in range(TILES):
            nc.vector.tensor_scalar(out=turns[:, 0, m, :], in0=freq[:], scalar1=token[:, m:m + 1],
                                    scalar2=1.0 / (2.0 * PI), op0=ALU.mult, op1=ALU.mult)
        nc.vector.tensor_scalar(out=turns[:, 1, :, :], in0=turns[:, 0, :, :], scalar1=0.25, scalar2=None, op0=ALU.add)
        turns_flat = turns[:].rearrange("p s m n -> p (s m n)")
        whole_i = const.tile([P, 2 * TILES * FREQS], I32, name="whole_i")
        nc.vector.tensor_copy(out=whole_i[:], in_=turns_flat)
        whole = const.tile([P, 2 * TILES * FREQS], F32, name="whole")
        nc.vector.tensor_copy(out=whole[:], in_=whole_i[:])
        rest = const.tile([P, 2 * TILES * FREQS], F32, name="rest")
        nc.vector.tensor_tensor(out=rest[:], in0=turns_flat, in1=whole[:], op=ALU.subtract)
        rest_neg = const.tile([P, 2 * TILES * FREQS], F32, name="rest_neg")
        nc.vector.scalar_tensor_tensor(out=rest_neg[:], in0=rest[:], scalar=0.5, in1=rest[:], op0=ALU.is_gt,
                                       op1=ALU.subtract)
        sin_cos = const.tile([P, 2, TILES, FREQS], F32, name="sin_cos")
        table = [const.tile([P, 2, 2, FREQS, 2], F32, name="table%d" % mp) for mp in range(2)]
        sign = const.tile([P, 2, 2], F32, name="sign")
        nc.vector.memset(sign[:], 1.0)
        nc.vector.memset(sign[:, 0, 1:2], -1.0)

        def take_sines():
            nc.scalar.activation(out=sin_cos[:].rearrange("p s m n -> p (s m n)"), in_=rest_neg[:], func=ACT.Sin,
                                 scale=-2.0 * PI)

        def spread_tables(mp):
            shape = [P, 2, 2 * FREQS, 2]
            (nc.gpsimd if PRM["spG"] else nc.vector).tensor_tensor(
                out=table[mp][:].rearrange("p s m n e -> p s (m n) e"),
                in0=sin_cos[:, :, 2 * mp:2 * mp + 2, :].rearrange("p s m n -> p s (m n)").unsqueeze(3).to_broadcast(shape),
                in1=sign[:].unsqueeze(2).to_broadcast(shape), op=ALU.mult)

        sorted_words = [None] * HEADS

        def sort_words(h, eng=None):
            sorted_words[h] = srt.tile([P, K // 2], F32, name="sorted")
            src = w_raw[h][:].bitcast(F32).rearrange("p (w u) -> p u w", u=2)
            dst = sorted_words[h][:].rearrange("p (u w) -> p u w", u=2)
            if eng is None:
                nc.vector.tensor_copy(out=dst, in_=src)
            elif eng is nc.scalar:
                nc.scalar.copy(out=dst, in_=src)
            else:
                nc.gpsimd.tensor_scalar(out=sorted_words[h][:].bitcast(BF16).rearrange("p (u w e) -> p u w e", u=2, e=2),
                                        in0=w_raw[h][:].rearrange("p (w u e) -> p u w e", u=2, e=2),
                                        scalar1=1.0, scalar2=0.0, op0=ALU.mult, op1=ALU.add)

        def turn_two_passes(rows, gp, grouped, presorted=None, eng=None):
            words = rows[:].bitcast(F32)
            bank = turned.tile([P, BANK], F32, name="bank")
            for gl in range(2):
                for u in range(2):
                    g = 2 * gp + gl
                    s = 2 * gl + u
                    if presorted is None:
                        nc.tensor.transpose(bank[:, s * P:(s + 1) * P], words[:, 256 * g + u:256 * (g + 1):2], ident[:])
                    else:
                        nc.tensor.transpose(bank[:, s * P:(s + 1) * P],
                                            presorted[:, 512 * u + P * g:512 * u + P * (g + 1)], ident[:])
            if eng is None:
                nc.scalar.copy(out=grouped, in_=bank[:].rearrange("p (g u r) -> p g r u", g=2, u=2))
            else:
                eng.tensor_copy(out=grouped, in_=bank[:].rearrange("p (g u r) -> p g r u", g=2, u=2))

        x_grouped = [None] * TILES
        x_codes = [keep.tile([P, PASSES * P], U32, name="x_codes%d" % m, align_bytes=64) for m in range(TILES)]
        x_scales = [keep.tile([P, PASSES * P], U8, name="x_scales%d" % m, align_bytes=64) for m in range(TILES)]

        def turn_x(m, gp, eng=None):
            if x_grouped[m] is None:
                x_grouped[m] = stage.tile([P, K], BF16, name="x_grouped", align_bytes=64)
            view = x_grouped[m][:].bitcast(F32).rearrange("p (g r u) -> p g r u", g=PASSES, u=2)
            turn_two_passes(x_raw[m], gp, view[:, 2 * gp:2 * gp + 2, :, :], None, eng)

        def quantize_x(m):
            nc.vector.quantize_mx(out=x_codes[m][:].bitcast(FP8X4), scales=x_scales[m][:], in_=x_grouped[m][:])

        w_grouped = [None] * PAIRS
        w_codes = [None] * PAIRS
        w_scales = [None] * PAIRS

        def turn_w(hp, gp, hl, eng=None):
            if w_grouped[hp] is None:
                w_grouped[hp] = stage.tile([P, 2 * K], BF16, name="w_grouped", align_bytes=64)
            view = w_grouped[hp][:].bitcast(F32).rearrange("p (g h d u) -> p g h d u", g=PASSES, h=2, u=2)
            turn_two_passes(w_raw[2 * hp + hl], gp, view[:, 2 * gp:2 * gp + 2, hl, :, :], sorted_words[2 * hp + hl], eng)

        def turn_half(q):
            for hl in range(2):
                turn_w(q // 2, q % 2, hl)

        def quantize_passes(hp, first, count):
            if w_codes[hp] is None:
                w_codes[hp] = stage.tile([P, PASSES * 2 * DH], U32, name="w_codes", align_bytes=64)
                w_scales[hp] = stage.tile([P, PASSES * 2 * DH], U8, name="w_scales", align_bytes=64)
            cols = slice(first * 2 * DH, (first + count) * 2 * DH)
            nc.vector.quantize_mx(out=w_codes[hp][:, cols].bitcast(FP8X4), scales=w_scales[hp][:, cols],
                                  in_=w_grouped[hp][:, first * 8 * DH:(first + count) * 8 * DH])

        out0_rows = out_0.rearrange("h (p m) d -> p h m d", m=TILES)
        out1_rows = out_1.rearrange("h (p m) d -> p h m d", m=TILES)
        acc = [None] * UNITS
        prod = {}
        rot = {}
        row_amax = {}
        factor = {}
        codes = {}

        def multiply(u):
            hp, mp = u // 2, u % 2
            acc[u] = sums.tile([P, BANK], F32, name="acc")
            for ml in range(2):
                m = 2 * mp + ml
                for g in range(PASSES):
                    nc.tensor.matmul_mx(out=acc[u][:, ml * 2 * DH:(ml + 1) * 2 * DH],
                                        lhsT=x_codes[m][:, g * P:(g + 1) * P].bitcast(FP8X4),
                                        lhsT_scale=x_scales[m][:, g * P:(g + 1) * P],
                                        rhs=w_codes[hp][:, g * 2 * DH:(g + 1) * 2 * DH].bitcast(FP8X4),
                                        rhs_scale=w_scales[hp][:, g * 2 * DH:(g + 1) * 2 * DH],
                                        start=(g == 0), stop=(g == PASSES - 1))

        def products(grp, k):
            u0, n = grp
            if k == 0:
                prod[grp] = prods.tile([P, n, 2, BANK], F32, name="prod%d" % n)
            u = u0 + k
            nc.vector.tensor_tensor(out=prod[grp][:, k, :, :].rearrange("p s (m h d) -> p s m h d", m=2, h=2),
                                    in0=acc[u][:].unsqueeze(1).to_broadcast([P, 2, BANK]).rearrange("p s (m h d) -> p s m h d", m=2, h=2),
                                    in1=table[u % 2][:].rearrange("p s m n e -> p s m (n e)").unsqueeze(3).to_broadcast([P, 2, 2, 2, DH]),
                                    op=ALU.mult)

        def products_gpsimd(grp, k):
            u = grp[0] + k
            if k == 0:
                prod[grp] = prods.tile([P, grp[1], 2, BANK], F32, name="prod%d" % grp[1])
            held = epi.tile([P, BANK], F32, name="held")
            nc.scalar.copy(out=held[:], in_=acc[u][:])
            nc.gpsimd.tensor_tensor(out=prod[grp][:, k, :, :].rearrange("p s (m h d) -> p s m h d", m=2, h=2),
                                    in0=held[:].unsqueeze(1).to_broadcast([P, 2, BANK]).rearrange("p s (m h d) -> p s m h d", m=2, h=2),
                                    in1=table[u % 2][:].rearrange("p s m n e -> p s m (n e)").unsqueeze(3).to_broadcast([P, 2, 2, 2, DH]),
                                    op=ALU.mult)

        def store_rows(grp, dst, src):
            u0, n = grp
            hp, m0 = u0 // 2, 2 * (u0 % 2)
            nc.sync.dma_start(out=dst[:, 2 * hp:2 * hp + 2, m0:m0 + 2 * n, :], in_=src.rearrange("p (h m d) -> p h m d", h=2, m=2 * n))

        def add_and_store(grp, eng=None):
            u0, n = grp
            rot[grp] = epi.tile([P, n * BANK], F32, name="rot%d" % n)
            pairs = "p k (m h n e) -> p k m h n e"
            (eng or nc.gpsimd).tensor_tensor(
                out=rot[grp][:].rearrange("p (h k m n e) -> p k m h n e", h=2, k=n, m=2, e=2),
                in0=prod[grp][:, :, 1, :].rearrange(pairs, m=2, h=2, e=2),
                in1=prod[grp][:, :, 0, :].rearrange(pairs, m=2, h=2, e=2)[:, :, :, :, :, ::-1],
                op=ALU.add)
            store_rows(grp, out0_rows, rot[grp][:])

        gate = const.tile([P, PAIRS], U32, name="gate")

        def gpsimd_waits_for_codes(hp):
            nc.gpsimd.tensor_copy(out=gate[:, hp:hp + 1], in_=w_codes[hp][:, 0:1])

        def add_one(grp, k, eng):
            n = grp[1]
            if k == 0:
                rot[grp] = epi.tile([P, n * BANK], F32, name="rot%d" % n)
            pairs = "p (m h n e) -> p m h n e"
            eng.tensor_tensor(
                out=rot[grp][:].rearrange("p (h k m n e) -> p k m h n e", h=2, k=n, m=2, e=2)[:, k, :, :, :, :],
                in0=prod[grp][:, k, 1, :].rearrange(pairs, m=2, h=2, e=2),
                in1=prod[grp][:, k, 0, :].rearrange(pairs, m=2, h=2, e=2)[:, :, :, :, ::-1],
                op=ALU.add)

        def take_row_amax(grp):
            n = grp[1]
            row_amax[grp] = epi.tile([P, 4 * n], F32, name="row_amax%d" % n)
            nc.vector.tensor_reduce(out=row_amax[grp][:], in_=rot[grp][:].rearrange("p (r d) -> p r d", d=DH),
                                    axis=AX.X, op=ALU.max, apply_absolute_value=True)

        def invert(grp):
            n = grp[1]
            factor[grp] = [epi.tile([P, 4 * n], F32, name="inverse%d" % n), None]
            nc.vector.reciprocal(out=factor[grp][0][:], in_=row_amax[grp][:])

        def make_factor(grp):
            n = grp[1]
            factor[grp][1] = epi.tile([P, 4 * n], F32, name="factor%d" % n)
            nc.scalar.activation(out=factor[grp][1][:], in_=factor[grp][0][:], func=ACT.Copy, scale=448.0)

        def cast_rows(grp, lo, hi, on_vector=False):
            n = grp[1]
            if grp not in codes:
                codes[grp] = epi.tile([P, n * BANK], FP8, name="codes%d" % n)
            for r in range(lo, hi):
                cols = slice(r * DH, (r + 1) * DH)
                if on_vector:
                    nc.vector.tensor_scalar(out=codes[grp][:, cols], in0=rot[grp][:, cols], scalar1=factor[grp][1][:, r:r + 1],
                                            scalar2=None, op0=ALU.mult, saturate=False)
                else:
                    nc.scalar.activation(out=codes[grp][:, cols], in_=rot[grp][:, cols], func=ACT.Identity,
                                         scale=factor[grp][1][:, r:r + 1], bias=zeros[:, 0:1], saturate=False)

        def store_codes(grp):
            store_rows(grp, out1_rows, codes[grp][:].bitcast(U8))

        V = nc.vector
        ENG = {"V": None, "V3": None, "S": nc.scalar, "G": nc.gpsimd}

        def at(h, e):
            if PRM.get(h) == e:
                sort_words(h, ENG[e])

        def turn_head(h, engs=(None, None)):
            for gp in range(2):
                turn_w(h // 2, gp, h % 2, engs[gp])

        G = [(2 * v, 2) for v in range(PAIRS)]
        def on(name):
            return V if name in PRM["vc"] else None

        turn_x(0, 0, on("x0a"))
        turn_x(0, 1, on("x0b"))
        quantize_x(0)
        turn_x(1, 0, on("x1a"))
        turn_x(1, 1, on("x1b"))
        quantize_x(1)
        take_sines()
        spread_tables(0)
        turn_head(0, (on("w0a"), on("w0b")))
        turn_head(1, (on("w1a"), on("w1b")))
        spread_tables(1)
        quantize_passes(0, 0, 2)
        quantize_passes(0, 2, 2)
        turn_x(2, 0, on("x2a"))
        turn_x(2, 1, on("x2b"))
        if PRM["mm0"] == 0:
            multiply(0)
        turn_x(3, 0, on("x3a"))
        turn_x(3, 1, on("x3b"))
        quantize_x(2)
        if PRM["mm0"] == 1:
            multiply(0)
        at(2, "V")
        turn_head(2)
        if PRM["p0"] == 0:
            products(G[0], 0)
        at(3, "S")
        at(3, "V3")
        quantize_x(3)
        at(3, "V")
        turn_head(3)
        multiply(1)
        at(4, "G")
        at(5, "G")
        at(6, "G")
        at(7, "G")
        at(8, "G")
        at(9, "G")
        if PRM["p0"] == 1:
            products(G[0], 0)
        at(4, "V")
        at(5, "V")
        if PRM["addV"] >= 1:
            add_one(G[0], 0, V)
        else:
            add_one(G[0], 0, nc.gpsimd)
        turn_head(5 if PRM["o2"] else 4)
        at(6, "S")
        turn_head(4 if PRM["o2"] else 5)
        at(7, "S")
        quantize_passes(1, 0, 4)
        products(G[0], 1)
        at(6, "V")
        at(7, "V")
        if PRM["addV"] >= 2:
            add_one(G[0], 1, V)
        multiply(2)
        multiply(3)
        quantize_passes(2, 0, 4)
        if PRM["fence"]:
            gpsimd_waits_for_codes(2)
        if PRM["addV"] < 2:
            add_one(G[0], 1, nc.gpsimd)
        store_rows(G[0], out0_rows, rot[G[0]][:])
        turn_head(7 if PRM["o3"] else 6)
        turn_head(6 if PRM["o3"] else 7)
        multiply(4)
        multiply(5)
        at(8, "S")
        at(9, "S")
        DR = 6
        turned_pairs = 4

        def turn_pair(hp):
            turn_half(2 * hp)
            turn_half(2 * hp + 1)

        for v in range(1, DR):
            if v not in PRM["gu"]:
                products(G[v], 0)
            if v + 1 in PRM["gu"] and PRM["gpos"] == 0:
                products_gpsimd(G[v + 1], 0)
            if v <= PRM["split"]:
                add_one(G[v], 0, nc.gpsimd)
            if v >= 2:
                invert(G[v - 2])
                make_factor(G[v - 2])
                cast_rows(G[v - 2], 0, 8)
                store_codes(G[v - 2])
            products(G[v], 1)
            if v <= PRM["redfirst"]:
                take_row_amax(G[v - 1])
            quantize_passes(v + 2, 0, 4)
            if PRM["fence"]:
                gpsimd_waits_for_codes(v + 2)
            if v <= PRM["split"]:
                add_one(G[v], 1, nc.gpsimd)
                store_rows(G[v], out0_rows, rot[G[v]][:])
            else:
                add_and_store(G[v])
            if v + 1 in PRM["gu"] and PRM["gpos"] == 1:
                products_gpsimd(G[v + 1], 0)
            if v > PRM["redfirst"]:
                take_row_amax(G[v - 1])
            while turned_pairs < PAIRS and turned_pairs <= (v + 4 if v >= PRM["deep"] else v + 3):
                turn_pair(turned_pairs)
                turned_pairs += 1
            multiply(2 * v + 4)
            multiply(2 * v + 5)
            for h in (2 * v + 8, 2 * v + 9):
                at(h, "S")
                at(h, "G")
        A, B, C, E = (12, 1), (13, 1), (14, 1), (15, 1)

        def finish(grp, on_vector=0):
            invert(grp)
            make_factor(grp)
            cast_rows(grp, 0, 4 * grp[1] - on_vector)
            if on_vector:
                cast_rows(grp, 4 * grp[1] - on_vector, 4 * grp[1], True)
            store_codes(grp)

        products(A, 0)
        add_and_store(A)
        finish(G[4])
        products(B, 0)
        add_and_store(B)
        take_row_amax(G[5])
        products(C, 0)
        add_and_store(C)
        finish(G[5])
        take_row_amax(A)
        products(E, 0)
        add_and_store(E)
        finish(A)
        take_row_amax(B)
        take_row_amax(C)
        finish(B)
        invert(C)
        make_factor(C)
        take_row_amax(E)
        invert(E)
        make_factor(E)
        cast_rows(C, 0, 4, True)
        store_codes(C)
        cast_rows(E, 0, 2)
        cast_rows(E, 2, 4, True)
        store_codes(E)
